import numpy as np
import ml_dtypes


def mxq(x, axis, fmt="e4m3"):
    dtype, down = {"e4m3": (ml_dtypes.float8_e4m3fn, 7), "e5m2": (ml_dtypes.float8_e5m2, 14)}[fmt]
    v = np.moveaxis(np.asarray(x, np.float32).astype(ml_dtypes.bfloat16).astype(np.float64), axis, -1)
    blocks = v.reshape(v.shape[:-1] + (-1, 32))
    amax = np.abs(blocks).max(-1, keepdims=True)
    byte = np.maximum(np.where(amax > 0, np.frexp(amax)[1] - 1 + 127, 0) - down, 1)
    scale = np.exp2(byte - 127.0)
    codes = (blocks / scale).astype(np.float32).astype(dtype).astype(np.float64)
    return np.moveaxis((codes * scale).reshape(v.shape), -1, axis)


WIDE = False


def mx_kscale(k):
    if not WIDE:
        return np.ones(k)
    levels = np.array([10, -10, 5, -5, 0])
    a = np.random.permutation(np.resize(levels, k // 512 * 4)).reshape(k // 512, 4)
    idx = np.arange(k)
    return np.exp2(a[idx // 512, idx % 128 // 32])


BF16 = ml_dtypes.bfloat16


def bf(x):
    return np.asarray(x, np.float32).astype(BF16)


def f64(x):
    return np.asarray(x).astype(np.float64)


M, K, N = 1024, 1024, 4096

THRESHOLD = 0.05
EPS = 1e-6


def ternarize_ste(weight):
    scale = np.maximum(np.mean(np.abs(weight)), EPS)
    t = THRESHOLD * scale
    ternary = np.where(weight > t, 1.0, np.where(weight < -t, -1.0, 0.0))
    return weight + (ternary - weight)


def setup_inputs():
    bound = 1.0 / np.sqrt(K)
    s = mx_kscale(K)
    r = s / s.min()
    keep = np.where(r <= 4.0, 1.0, 2.0 ** -20)
    return {"x": bf(np.random.standard_normal((M, K)) * 4.0 / np.sqrt(K) * r[None, :]),
            "weight": bf(np.random.uniform(-bound, bound, (N, K)) * keep[None, :]),
            "bias": bf(np.random.standard_normal(N) * 0.5)}


def reference(x, weight, bias):
    q_weight = ternarize_ste(f64(weight))
    return (mxq(f64(x), 1, "e4m3") @ mxq(q_weight, 1, "e4m3").T) + f64(bias)

@@ -1,0 +1,212 @@
+from contextlib import ExitStack
+
+import concourse.mybir as mybir
+from concourse.masks import make_identity
+
+F32 = mybir.dt.float32
+BF16 = mybir.dt.bfloat16
+I32 = mybir.dt.int32
+U32 = mybir.dt.uint32
+U8 = mybir.dt.uint8
+FP8X4 = mybir.dt.float8_e4m3fn_x4
+ALU = mybir.AluOpType
+ACT = mybir.ActivationFunctionType
+
+P = 128
+M, K, N = 1024, 1024, 4096
+FLOPS = 2 * M * K * N
+
+THRESHOLD = 0.05
+EPS = 1e-6
+
+GROUP = 512
+BLOCKS = GROUP // P
+PASSES = K // 512
+WORDS = K // 2
+N_GROUPS = N // GROUP
+M_GROUPS = M // GROUP
+
+SCALAR_TILES = 3
+
+ABS_BITS = 0x7FFF7FFF
+SIGN_BITS = -0x7FFF8000
+
+
+def flat(ap):
+    return ap.rearrange("p b k -> p (b k)")
+
+
+def transpose_group(nc, psum_t, grouped_pool, rows, ident):
+    grouped = grouped_pool.tile([P, PASSES, GROUP, 2], F32, tag="grouped", align_bytes=64)
+    for g in range(PASSES):
+        for half in range(BLOCKS // 2):
+            bank = psum_t.tile([P, 2, 2, P], F32, tag="tp")
+            for b in range(2):
+                words = rows[:, 2 * half + b, :].bitcast(F32)
+                for u in range(2):
+                    first = (2 * g + u) * P
+                    nc.tensor.transpose(bank[:, b, u, :], words[:, first : first + P], ident[:])
+            nc.scalar.copy(
+                out=grouped[:, g, 2 * P * half : 2 * P * (half + 1), :].rearrange(
+                    "p (b r) u -> p b r u", b=2
+                ),
+                in_=bank[:].rearrange("p b u r -> p b r u"),
+            )
+    return grouped
+
+
+def quantise_group(nc, grouped, codes, scales):
+    nc.vector.quantize_mx(
+        out=codes[:].rearrange("p g r -> p (g r)").bitcast(FP8X4),
+        scales=scales[:].rearrange("p g r -> p (g r)"),
+        in_=grouped[:].rearrange("p g r u -> p (g r u)").bitcast(BF16),
+    )
+
+
+def tile_bitlinear_kernel(tc, x, weight, bias, out):
+    nc = tc.nc
+    with ExitStack() as ctx:
+        keep = ctx.enter_context(tc.tile_pool(name="keep", bufs=1))
+        grouped_pool = ctx.enter_context(tc.tile_pool(name="grouped", bufs=2))
+        q_pool = ctx.enter_context(tc.tile_pool(name="q", bufs=2))
+        res_pool = ctx.enter_context(tc.tile_pool(name="res", bufs=6))
+        raw_pool = ctx.enter_context(tc.tile_pool(name="raw", bufs=3))
+        psum_t = ctx.enter_context(tc.psum_pool(name="psum_t", bufs=4))
+        psum_o = ctx.enter_context(tc.psum_pool(name="psum_o", bufs=4))
+        ctx.enter_context(tc.manual_schedule())
+
+        ident = keep.tile([P, P], F32)
+        make_identity(nc, ident[:])
+        ones = keep.tile([P, P], F32)
+        nc.vector.memset(ones[:], 1.0)
+
+        w_rows = [keep.tile([P, BLOCKS, K], BF16, name="w%d" % j) for j in range(N_GROUPS)]
+        w_abs = [keep.tile([P, BLOCKS, K], BF16, name="a%d" % j) for j in range(N_GROUPS)]
+        w_view = weight.rearrange("(j h b p) k -> j h p b k", j=N_GROUPS, h=2, p=P)
+        for j in range(N_GROUPS):
+            for h in range(2):
+                nc.sync.dma_start(out=w_rows[j][:, 2 * h : 2 * h + 2, :], in_=w_view[j, h])
+        x_rows = [keep.tile([P, BLOCKS, K], BF16, name="x%d" % i) for i in range(M_GROUPS)]
+        x_view = x.rearrange("(i b p) k -> i p b k", i=M_GROUPS, p=P)
+        for i in range(M_GROUPS):
+            nc.sync.dma_start(out=x_rows[i][:], in_=x_view[i])
+        bias_all = keep.tile([P, N], BF16)
+        nc.sync.dma_start(out=bias_all[:], in_=bias.partition_broadcast(P))
+
+        sum_scalar = keep.tile([P, N_GROUPS], F32)
+        sum_vector = keep.tile([P, N_GROUPS], F32)
+        for j in range(N_GROUPS):
+            nc.scalar.activation(
+                out=w_abs[j][:, 0:2, :],
+                in_=w_rows[j][:, 0:2, :],
+                func=ACT.Abs,
+                accum_out=sum_scalar[:, j : j + 1],
+            )
+            nc.vector.tensor_scalar(
+                out=flat(w_abs[j][:, 2:4, :]).bitcast(I32),
+                in0=flat(w_rows[j][:, 2:4, :]).bitcast(I32),
+                scalar1=ABS_BITS,
+                scalar2=None,
+                op0=ALU.bitwise_and,
+            )
+            nc.vector.tensor_scalar(
+                out=flat(w_abs[j][:, 2:4, :]),
+                in0=flat(w_abs[j][:, 2:4, :]),
+                scalar1=0.0,
+                scalar2=None,
+                op0=ALU.max,
+                op1=ALU.add,
+                accum_out=sum_vector[:, j : j + 1],
+            )
+
+        total_ps = psum_t.tile([P, N_GROUPS], F32, tag="tp")
+        nc.tensor.matmul(total_ps[:], lhsT=ones[:], rhs=sum_scalar[:], start=True, stop=False)
+        nc.tensor.matmul(total_ps[:], lhsT=ones[:], rhs=sum_vector[:], start=False, stop=True)
+        total = keep.tile([P, 1], F32)
+        nc.vector.tensor_reduce(out=total[:], in_=total_ps[:], axis=mybir.AxisListType.X, op=ALU.add)
+        scale = keep.tile([P, 1], F32)
+        nc.vector.tensor_scalar(
+            out=scale[:], in0=total[:], scalar1=1.0 / (N * K), scalar2=EPS, op0=ALU.mult, op1=ALU.max
+        )
+        thr = keep.tile([P, 1], F32)
+        nc.vector.tensor_scalar(
+            out=thr[:], in0=scale[:], scalar1=THRESHOLD, scalar2=None, op0=ALU.mult
+        )
+
+        def ternarise(j):
+            nc.vector.tensor_scalar(
+                out=flat(w_abs[j][:]),
+                in0=flat(w_abs[j][:]),
+                scalar1=thr[:, 0:1],
+                scalar2=None,
+                op0=ALU.is_gt,
+            )
+            nc.vector.scalar_tensor_tensor(
+                out=flat(w_rows[j][:]).bitcast(I32),
+                in0=flat(w_rows[j][:]).bitcast(I32),
+                scalar=SIGN_BITS,
+                in1=flat(w_abs[j][:]).bitcast(I32),
+                op0=ALU.bitwise_and,
+                op1=ALU.bitwise_or,
+            )
+
+        q_grouped = {}
+        q_codes = {}
+        q_scales = {}
+
+        def transpose_q(j):
+            q_grouped[j] = transpose_group(nc, psum_t, grouped_pool, w_rows[j], ident)
+
+        def quantise_q(j):
+            codes = q_pool.tile([P, PASSES, GROUP], U32, tag="codes", align_bytes=64)
+            scales = q_pool.tile([P, PASSES, GROUP], U8, tag="scales", align_bytes=64)
+            quantise_group(nc, q_grouped[j], codes, scales)
+            q_codes[j] = codes
+            q_scales[j] = scales
+
+        x_codes = [keep.tile([P, PASSES, GROUP], U32, name="xc%d" % i, align_bytes=64) for i in range(M_GROUPS)]
+        x_scales = [keep.tile([P, PASSES, GROUP], U8, name="xs%d" % i, align_bytes=64) for i in range(M_GROUPS)]
+
+        def multiply(j):
+            cols = slice(GROUP * j, GROUP * (j + 1))
+            for i in range(M_GROUPS):
+                for b in range(BLOCKS):
+                    rows = slice(P * b, P * (b + 1))
+                    acc = psum_o.tile([P, GROUP], F32, tag="acc")
+                    for g in range(PASSES):
+                        nc.tensor.matmul_mx(
+                            out=acc[:],
+                            lhsT=x_codes[i][:, g, rows].bitcast(FP8X4),
+                            lhsT_scale=x_scales[i][:, g, rows],
+                            rhs=q_codes[j][:, g, :].bitcast(FP8X4),
+                            rhs_scale=q_scales[j][:, g, :],
+                            start=(g == 0),
+                            stop=(g == PASSES - 1),
+                        )
+                    res = res_pool.tile([P, GROUP], F32, tag="res")
+                    if BLOCKS * i + b < SCALAR_TILES:
+                        raw = raw_pool.tile([P, GROUP], F32, tag="raw")
+                        nc.scalar.copy(out=raw[:], in_=acc[:])
+                        nc.gpsimd.tensor_tensor(out=res[:], in0=raw[:], in1=bias_all[:, cols], op=ALU.add)
+                    else:
+                        nc.vector.tensor_tensor(out=res[:], in0=acc[:], in1=bias_all[:, cols], op=ALU.add)
+                    first = GROUP * i + P * b
+                    nc.sync.dma_start(out=out[first : first + P, cols], in_=res[:])
+
+        ternarise(0)
+        ternarise(1)
+        for i in range(M_GROUPS):
+            x_grouped = transpose_group(nc, psum_t, grouped_pool, x_rows[i], ident)
+            quantise_group(nc, x_grouped, x_codes[i], x_scales[i])
+        transpose_q(0)
+        quantise_q(0)
+        transpose_q(1)
+        ternarise(2)
+        for j in range(N_GROUPS):
+            if j + 3 < N_GROUPS:
+                ternarise(j + 3)
+            if j + 1 < N_GROUPS:
+                quantise_q(j + 1)
+            multiply(j)
+            if j + 2 < N_GROUPS:
+                transpose_q(j + 2)

@@ -26,7 +26,7 @@ WORDS = K // 2
 N_GROUPS = N // GROUP
 M_GROUPS = M // GROUP
 
-SCALAR_TILES = 3
+SCALAR_TILES = 0
 
 ABS_BITS = 0x7FFF7FFF
 SIGN_BITS = -0x7FFF8000

@@ -20,37 +20,50 @@ THRESHOLD = 0.05
 EPS = 1e-6
 
 GROUP = 512
-BLOCKS = GROUP // P
+HALF = GROUP // 2
 PASSES = K // 512
-WORDS = K // 2
 N_GROUPS = N // GROUP
 M_GROUPS = M // GROUP
 
-SCALAR_TILES = 0
-
 ABS_BITS = 0x7FFF7FFF
 SIGN_BITS = -0x7FFF8000
+TOP_BITS = -0x10000
+MID_BIT = 0x8000
+ROUND = 12582912.0
+
+SCALAR_FROM = 2
 
 
 def flat(ap):
     return ap.rearrange("p b k -> p (b k)")
 
 
-def transpose_group(nc, psum_t, grouped_pool, rows, ident):
+def load_halves(nc, pool, dram, groups, name):
+    view = dram.rearrange("(j h p b) k -> j h p (b k)", j=groups, h=2, p=P)
+    tiles = []
+    for j in range(groups):
+        pair = []
+        for h in range(2):
+            rows = pool.tile([P, 2, K], BF16, name="%s%d_%d" % (name, j, h))
+            nc.sync.dma_start(out=flat(rows[:]), in_=view[j, h])
+            pair.append(rows)
+        tiles.append(pair)
+    return tiles
+
+
+def transpose_group(nc, psum_t, grouped_pool, halves, ident):
     grouped = grouped_pool.tile([P, PASSES, GROUP, 2], F32, tag="grouped", align_bytes=64)
-    for g in range(PASSES):
-        for half in range(BLOCKS // 2):
+    for h in (1, 0):
+        for g in range(PASSES):
             bank = psum_t.tile([P, 2, 2, P], F32, tag="tp")
             for b in range(2):
-                words = rows[:, 2 * half + b, :].bitcast(F32)
+                words = halves[h][:, b, :].bitcast(F32)
                 for u in range(2):
                     first = (2 * g + u) * P
                     nc.tensor.transpose(bank[:, b, u, :], words[:, first : first + P], ident[:])
             nc.scalar.copy(
-                out=grouped[:, g, 2 * P * half : 2 * P * (half + 1), :].rearrange(
-                    "p (b r) u -> p b r u", b=2
-                ),
-                in_=bank[:].rearrange("p b u r -> p b r u"),
+                out=grouped[:, g, HALF * h : HALF * (h + 1), :].rearrange("p (r b) u -> p r b u", b=2),
+                in_=bank[:].rearrange("p b u r -> p r b u"),
             )
     return grouped
 
@@ -68,9 +81,9 @@ def tile_bitlinear_kernel(tc, x, weight, bias, out):
     with ExitStack() as ctx:
         keep = ctx.enter_context(tc.tile_pool(name="keep", bufs=1))
         grouped_pool = ctx.enter_context(tc.tile_pool(name="grouped", bufs=2))
+        rounded_pool = ctx.enter_context(tc.tile_pool(name="rounded", bufs=2))
         q_pool = ctx.enter_context(tc.tile_pool(name="q", bufs=2))
         res_pool = ctx.enter_context(tc.tile_pool(name="res", bufs=6))
-        raw_pool = ctx.enter_context(tc.tile_pool(name="raw", bufs=3))
         psum_t = ctx.enter_context(tc.psum_pool(name="psum_t", bufs=4))
         psum_o = ctx.enter_context(tc.psum_pool(name="psum_o", bufs=4))
         ctx.enter_context(tc.manual_schedule())
@@ -79,39 +92,37 @@ def tile_bitlinear_kernel(tc, x, weight, bias, out):
         make_identity(nc, ident[:])
         ones = keep.tile([P, P], F32)
         nc.vector.memset(ones[:], 1.0)
+        minus_round = keep.tile([P, 1], F32)
+        nc.vector.memset(minus_round[:], -ROUND)
 
-        w_rows = [keep.tile([P, BLOCKS, K], BF16, name="w%d" % j) for j in range(N_GROUPS)]
-        w_abs = [keep.tile([P, BLOCKS, K], BF16, name="a%d" % j) for j in range(N_GROUPS)]
-        w_view = weight.rearrange("(j h b p) k -> j h p b k", j=N_GROUPS, h=2, p=P)
-        for j in range(N_GROUPS):
-            for h in range(2):
-                nc.sync.dma_start(out=w_rows[j][:, 2 * h : 2 * h + 2, :], in_=w_view[j, h])
-        x_rows = [keep.tile([P, BLOCKS, K], BF16, name="x%d" % i) for i in range(M_GROUPS)]
-        x_view = x.rearrange("(i b p) k -> i p b k", i=M_GROUPS, p=P)
-        for i in range(M_GROUPS):
-            nc.sync.dma_start(out=x_rows[i][:], in_=x_view[i])
+        w_rows = load_halves(nc, keep, weight, N_GROUPS, "w")
+        x_rows = load_halves(nc, keep, x, M_GROUPS, "x")
         bias_all = keep.tile([P, N], BF16)
         nc.sync.dma_start(out=bias_all[:], in_=bias.partition_broadcast(P))
 
+        w_abs = [
+            [keep.tile([P, 2, K], BF16, name="a%d_%d" % (j, h)) for h in range(2)]
+            for j in range(N_GROUPS)
+        ]
         sum_scalar = keep.tile([P, N_GROUPS], F32)
         sum_vector = keep.tile([P, N_GROUPS], F32)
         for j in range(N_GROUPS):
             nc.scalar.activation(
-                out=w_abs[j][:, 0:2, :],
-                in_=w_rows[j][:, 0:2, :],
+                out=w_abs[j][0][:],
+                in_=w_rows[j][0][:],
                 func=ACT.Abs,
                 accum_out=sum_scalar[:, j : j + 1],
             )
             nc.vector.tensor_scalar(
-                out=flat(w_abs[j][:, 2:4, :]).bitcast(I32),
-                in0=flat(w_rows[j][:, 2:4, :]).bitcast(I32),
+                out=flat(w_abs[j][1][:]).bitcast(I32),
+                in0=flat(w_rows[j][1][:]).bitcast(I32),
                 scalar1=ABS_BITS,
                 scalar2=None,
                 op0=ALU.bitwise_and,
             )
             nc.vector.tensor_scalar(
-                out=flat(w_abs[j][:, 2:4, :]),
-                in0=flat(w_abs[j][:, 2:4, :]),
+                out=flat(w_abs[j][1][:]),
+                in0=flat(w_abs[j][1][:]),
                 scalar1=0.0,
                 scalar2=None,
                 op0=ALU.max,
@@ -132,23 +143,58 @@ def tile_bitlinear_kernel(tc, x, weight, bias, out):
         nc.vector.tensor_scalar(
             out=thr[:], in0=scale[:], scalar1=THRESHOLD, scalar2=None, op0=ALU.mult
         )
+        mid = keep.tile([P, 1], F32)
+        nc.vector.tensor_scalar(
+            out=mid[:].bitcast(I32),
+            in0=thr[:].bitcast(I32),
+            scalar1=TOP_BITS,
+            scalar2=MID_BIT,
+            op0=ALU.bitwise_and,
+            op1=ALU.bitwise_or,
+        )
+        twice_mid = keep.tile([P, 1], F32)
+        nc.vector.tensor_scalar(
+            out=twice_mid[:], in0=mid[:], scalar1=2.0, scalar2=None, op0=ALU.mult
+        )
+        inv_twice_mid = keep.tile([P, 1], F32)
+        nc.vector.reciprocal(out=inv_twice_mid[:], in_=twice_mid[:])
 
-        def ternarise(j):
+        def ternarise_on_vector(j, h):
             nc.vector.tensor_scalar(
-                out=flat(w_abs[j][:]),
-                in0=flat(w_abs[j][:]),
+                out=flat(w_abs[j][h][:]),
+                in0=flat(w_abs[j][h][:]),
                 scalar1=thr[:, 0:1],
                 scalar2=None,
                 op0=ALU.is_gt,
             )
             nc.vector.scalar_tensor_tensor(
-                out=flat(w_rows[j][:]).bitcast(I32),
-                in0=flat(w_rows[j][:]).bitcast(I32),
+                out=flat(w_rows[j][h][:]).bitcast(I32),
+                in0=flat(w_rows[j][h][:]).bitcast(I32),
                 scalar=SIGN_BITS,
-                in1=flat(w_abs[j][:]).bitcast(I32),
+                in1=flat(w_abs[j][h][:]).bitcast(I32),
                 op0=ALU.bitwise_and,
                 op1=ALU.bitwise_or,
             )
+
+        def ternarise_on_scalar(j, h):
+            rounded = rounded_pool.tile([P, 2, K], F32, tag="rounded")
+            nc.scalar.activation(
+                out=rounded[:],
+                in_=w_rows[j][h][:],
+                func=ACT.Copy,
+                scale=inv_twice_mid[:, 0:1],
+                bias=ROUND,
+            )
+            nc.scalar.activation(
+                out=w_rows[j][h][:], in_=rounded[:], func=ACT.Sign, bias=minus_round[:, 0:1]
+            )
+
+        def ternarise(j):
+            ternarise_on_vector(j, 1)
+            if j < SCALAR_FROM:
+                ternarise_on_vector(j, 0)
+            else:
+                ternarise_on_scalar(j, 0)
 
         q_grouped = {}
         q_codes = {}
@@ -164,34 +210,32 @@ def tile_bitlinear_kernel(tc, x, weight, bias, out):
             q_codes[j] = codes
             q_scales[j] = scales
 
-        x_codes = [keep.tile([P, PASSES, GROUP], U32, name="xc%d" % i, align_bytes=64) for i in range(M_GROUPS)]
-        x_scales = [keep.tile([P, PASSES, GROUP], U8, name="xs%d" % i, align_bytes=64) for i in range(M_GROUPS)]
+        x_codes = [
+            keep.tile([P, PASSES, GROUP], U32, name="xc%d" % i, align_bytes=64) for i in range(M_GROUPS)
+        ]
+        x_scales = [
+            keep.tile([P, PASSES, GROUP], U8, name="xs%d" % i, align_bytes=64) for i in range(M_GROUPS)
+        ]
 
-        def multiply(j):
+        def multiply(j, i):
             cols = slice(GROUP * j, GROUP * (j + 1))
-            for i in range(M_GROUPS):
-                for b in range(BLOCKS):
-                    rows = slice(P * b, P * (b + 1))
-                    acc = psum_o.tile([P, GROUP], F32, tag="acc")
-                    for g in range(PASSES):
-                        nc.tensor.matmul_mx(
-                            out=acc[:],
-                            lhsT=x_codes[i][:, g, rows].bitcast(FP8X4),
-                            lhsT_scale=x_scales[i][:, g, rows],
-                            rhs=q_codes[j][:, g, :].bitcast(FP8X4),
-                            rhs_scale=q_scales[j][:, g, :],
-                            start=(g == 0),
-                            stop=(g == PASSES - 1),
-                        )
-                    res = res_pool.tile([P, GROUP], F32, tag="res")
-                    if BLOCKS * i + b < SCALAR_TILES:
-                        raw = raw_pool.tile([P, GROUP], F32, tag="raw")
-                        nc.scalar.copy(out=raw[:], in_=acc[:])
-                        nc.gpsimd.tensor_tensor(out=res[:], in0=raw[:], in1=bias_all[:, cols], op=ALU.add)
-                    else:
-                        nc.vector.tensor_tensor(out=res[:], in0=acc[:], in1=bias_all[:, cols], op=ALU.add)
-                    first = GROUP * i + P * b
-                    nc.sync.dma_start(out=out[first : first + P, cols], in_=res[:])
+            for s in range(GROUP // P):
+                rows = slice(P * s, P * (s + 1))
+                acc = psum_o.tile([P, GROUP], F32, tag="acc")
+                for g in range(PASSES):
+                    nc.tensor.matmul_mx(
+                        out=acc[:],
+                        lhsT=x_codes[i][:, g, rows].bitcast(FP8X4),
+                        lhsT_scale=x_scales[i][:, g, rows],
+                        rhs=q_codes[j][:, g, :].bitcast(FP8X4),
+                        rhs_scale=q_scales[j][:, g, :],
+                        start=(g == 0),
+                        stop=(g == PASSES - 1),
+                    )
+                res = res_pool.tile([P, GROUP], F32, tag="res")
+                nc.vector.tensor_tensor(out=res[:], in0=acc[:], in1=bias_all[:, cols], op=ALU.add)
+                first = GROUP * i + P * s
+                nc.sync.dma_start(out=out[first : first + P, cols], in_=res[:])
 
         ternarise(0)
         ternarise(1)
@@ -201,12 +245,12 @@ def tile_bitlinear_kernel(tc, x, weight, bias, out):
         transpose_q(0)
         quantise_q(0)
         transpose_q(1)
-        ternarise(2)
         for j in range(N_GROUPS):
-            if j + 3 < N_GROUPS:
-                ternarise(j + 3)
+            if j + 2 < N_GROUPS:
+                ternarise(j + 2)
+            multiply(j, 0)
             if j + 1 < N_GROUPS:
                 quantise_q(j + 1)
-            multiply(j)
+            multiply(j, 1)
             if j + 2 < N_GROUPS:
                 transpose_q(j + 2)

@@ -80,18 +80,18 @@ def tile_bitlinear_kernel(tc, x, weight, bias, out):
     nc = tc.nc
     with ExitStack() as ctx:
         keep = ctx.enter_context(tc.tile_pool(name="keep", bufs=1))
-        grouped_pool = ctx.enter_context(tc.tile_pool(name="grouped", bufs=2))
-        rounded_pool = ctx.enter_context(tc.tile_pool(name="rounded", bufs=2))
+        grouped_pool = ctx.enter_context(tc.tile_pool(name="grouped", bufs=3))
+        rounded_pool = ctx.enter_context(tc.tile_pool(name="rounded", bufs=1))
         q_pool = ctx.enter_context(tc.tile_pool(name="q", bufs=2))
-        res_pool = ctx.enter_context(tc.tile_pool(name="res", bufs=6))
+        res_pool = ctx.enter_context(tc.tile_pool(name="res", bufs=8))
         psum_t = ctx.enter_context(tc.psum_pool(name="psum_t", bufs=4))
         psum_o = ctx.enter_context(tc.psum_pool(name="psum_o", bufs=4))
         ctx.enter_context(tc.manual_schedule())
 
         ident = keep.tile([P, P], F32)
         make_identity(nc, ident[:])
-        ones = keep.tile([P, P], F32)
-        nc.vector.memset(ones[:], 1.0)
+        averager = keep.tile([P, P], F32)
+        nc.vector.memset(averager[:], 1.0 / (N * K))
         minus_round = keep.tile([P, 1], F32)
         nc.vector.memset(minus_round[:], -ROUND)
 
@@ -130,36 +130,40 @@ def tile_bitlinear_kernel(tc, x, weight, bias, out):
                 accum_out=sum_vector[:, j : j + 1],
             )
 
-        total_ps = psum_t.tile([P, N_GROUPS], F32, tag="tp")
-        nc.tensor.matmul(total_ps[:], lhsT=ones[:], rhs=sum_scalar[:], start=True, stop=False)
-        nc.tensor.matmul(total_ps[:], lhsT=ones[:], rhs=sum_vector[:], start=False, stop=True)
-        total = keep.tile([P, 1], F32)
-        nc.vector.tensor_reduce(out=total[:], in_=total_ps[:], axis=mybir.AxisListType.X, op=ALU.add)
-        scale = keep.tile([P, 1], F32)
-        nc.vector.tensor_scalar(
-            out=scale[:], in0=total[:], scalar1=1.0 / (N * K), scalar2=EPS, op0=ALU.mult, op1=ALU.max
-        )
+        mean_ps = psum_t.tile([P, N_GROUPS], F32, tag="tp")
+        nc.tensor.matmul(mean_ps[:], lhsT=averager[:], rhs=sum_scalar[:], start=True, stop=False)
+        nc.tensor.matmul(mean_ps[:], lhsT=averager[:], rhs=sum_vector[:], start=False, stop=True)
+        mean = keep.tile([P, 1], F32)
+        nc.vector.tensor_reduce(out=mean[:], in_=mean_ps[:], axis=mybir.AxisListType.X, op=ALU.add)
         thr = keep.tile([P, 1], F32)
         nc.vector.tensor_scalar(
-            out=thr[:], in0=scale[:], scalar1=THRESHOLD, scalar2=None, op0=ALU.mult
+            out=thr[:], in0=mean[:], scalar1=EPS, scalar2=THRESHOLD, op0=ALU.max, op1=ALU.mult
         )
         mid = keep.tile([P, 1], F32)
-        nc.vector.tensor_scalar(
-            out=mid[:].bitcast(I32),
-            in0=thr[:].bitcast(I32),
-            scalar1=TOP_BITS,
-            scalar2=MID_BIT,
-            op0=ALU.bitwise_and,
-            op1=ALU.bitwise_or,
-        )
         twice_mid = keep.tile([P, 1], F32)
-        nc.vector.tensor_scalar(
-            out=twice_mid[:], in0=mid[:], scalar1=2.0, scalar2=None, op0=ALU.mult
-        )
         inv_twice_mid = keep.tile([P, 1], F32)
-        nc.vector.reciprocal(out=inv_twice_mid[:], in_=twice_mid[:])
 
-        def ternarise_on_vector(j, h):
+        def prepare_rounding():
+            nc.vector.tensor_scalar(
+                out=mid[:].bitcast(I32),
+                in0=thr[:].bitcast(I32),
+                scalar1=TOP_BITS,
+                scalar2=MID_BIT,
+                op0=ALU.bitwise_and,
+                op1=ALU.bitwise_or,
+            )
+            nc.vector.tensor_scalar(
+                out=twice_mid[:], in0=mid[:], scalar1=2.0, scalar2=None, op0=ALU.mult
+            )
+            nc.vector.reciprocal(out=inv_twice_mid[:], in_=twice_mid[:])
+
+        def ternarise_on_vector(j, halves):
+            for h in halves:
+                compare(j, h)
+            for h in halves:
+                put_sign(j, h)
+
+        def compare(j, h):
             nc.vector.tensor_scalar(
                 out=flat(w_abs[j][h][:]),
                 in0=flat(w_abs[j][h][:]),
@@ -167,6 +171,8 @@ def tile_bitlinear_kernel(tc, x, weight, bias, out):
                 scalar2=None,
                 op0=ALU.is_gt,
             )
+
+        def put_sign(j, h):
             nc.vector.scalar_tensor_tensor(
                 out=flat(w_rows[j][h][:]).bitcast(I32),
                 in0=flat(w_rows[j][h][:]).bitcast(I32),
@@ -190,10 +196,10 @@ def tile_bitlinear_kernel(tc, x, weight, bias, out):
             )
 
         def ternarise(j):
-            ternarise_on_vector(j, 1)
             if j < SCALAR_FROM:
-                ternarise_on_vector(j, 0)
+                ternarise_on_vector(j, (1, 0))
             else:
+                ternarise_on_vector(j, (1,))
                 ternarise_on_scalar(j, 0)
 
         q_grouped = {}
@@ -239,6 +245,7 @@ def tile_bitlinear_kernel(tc, x, weight, bias, out):
 
         ternarise(0)
         ternarise(1)
+        prepare_rounding()
         for i in range(M_GROUPS):
             x_grouped = transpose_group(nc, psum_t, grouped_pool, x_rows[i], ident)
             quantise_group(nc, x_grouped, x_codes[i], x_scales[i])

@@ -19,245 +19,256 @@ FLOPS = 2 * M * K * N
 THRESHOLD = 0.05
 EPS = 1e-6
 
-GROUP = 512
-HALF = GROUP // 2
+PIECE = 2 * P
 PASSES = K // 512
-N_GROUPS = N // GROUP
-M_GROUPS = M // GROUP
+X_GROUP = 512
+X_GROUPS = M // X_GROUP
+CHUNKS = [256, 256, 512, 512, 512, 512, 512, 512, 512]
+N_PIECES = N // PIECE
 
 ABS_BITS = 0x7FFF7FFF
-SIGN_BITS = -0x7FFF8000
+TWO_BITS = -0x3FFF4000
 TOP_BITS = -0x10000
-MID_BIT = 0x8000
-ROUND = 12582912.0
-
-SCALAR_FROM = 2
+THREE_QUARTERS = 0xC000
+SUM_COLS = 256
 
 
 def flat(ap):
-    return ap.rearrange("p b k -> p (b k)")
+    return ap.rearrange("p a k -> p (a k)")
 
 
-def load_halves(nc, pool, dram, groups, name):
-    view = dram.rearrange("(j h p b) k -> j h p (b k)", j=groups, h=2, p=P)
-    tiles = []
-    for j in range(groups):
-        pair = []
-        for h in range(2):
-            rows = pool.tile([P, 2, K], BF16, name="%s%d_%d" % (name, j, h))
-            nc.sync.dma_start(out=flat(rows[:]), in_=view[j, h])
-            pair.append(rows)
-        tiles.append(pair)
-    return tiles
-
-
-def transpose_group(nc, psum_t, grouped_pool, halves, ident):
-    grouped = grouped_pool.tile([P, PASSES, GROUP, 2], F32, tag="grouped", align_bytes=64)
-    for h in (1, 0):
-        for g in range(PASSES):
-            bank = psum_t.tile([P, 2, 2, P], F32, tag="tp")
-            for b in range(2):
-                words = halves[h][:, b, :].bitcast(F32)
-                for u in range(2):
-                    first = (2 * g + u) * P
-                    nc.tensor.transpose(bank[:, b, u, :], words[:, first : first + P], ident[:])
-            nc.scalar.copy(
-                out=grouped[:, g, HALF * h : HALF * (h + 1), :].rearrange("p (r b) u -> p r b u", b=2),
-                in_=bank[:].rearrange("p b u r -> p r b u"),
-            )
-    return grouped
-
-
-def quantise_group(nc, grouped, codes, scales):
-    nc.vector.quantize_mx(
-        out=codes[:].rearrange("p g r -> p (g r)").bitcast(FP8X4),
-        scales=scales[:].rearrange("p g r -> p (g r)"),
-        in_=grouped[:].rearrange("p g r u -> p (g r u)").bitcast(BF16),
-    )
+def words4(ap):
+    return ap.rearrange("p a c t -> p (a c t)")
 
 
 def tile_bitlinear_kernel(tc, x, weight, bias, out):
     nc = tc.nc
     with ExitStack() as ctx:
         keep = ctx.enter_context(tc.tile_pool(name="keep", bufs=1))
-        grouped_pool = ctx.enter_context(tc.tile_pool(name="grouped", bufs=3))
-        rounded_pool = ctx.enter_context(tc.tile_pool(name="rounded", bufs=1))
+        abs_pool = ctx.enter_context(tc.tile_pool(name="absolute", bufs=4))
         q_pool = ctx.enter_context(tc.tile_pool(name="q", bufs=2))
         res_pool = ctx.enter_context(tc.tile_pool(name="res", bufs=8))
-        psum_t = ctx.enter_context(tc.psum_pool(name="psum_t", bufs=4))
-        psum_o = ctx.enter_context(tc.psum_pool(name="psum_o", bufs=4))
+        psum = ctx.enter_context(tc.psum_pool(name="psum", bufs=7))
+        psum_s = ctx.enter_context(tc.psum_pool(name="psum_s", bufs=1))
         ctx.enter_context(tc.manual_schedule())
 
         ident = keep.tile([P, P], F32)
         make_identity(nc, ident[:])
         averager = keep.tile([P, P], F32)
         nc.vector.memset(averager[:], 1.0 / (N * K))
-        minus_round = keep.tile([P, 1], F32)
-        nc.vector.memset(minus_round[:], -ROUND)
+        averager_b = keep.tile([P, P], BF16)
+        nc.vector.memset(averager_b[:], 1.0 / (N * K))
 
-        w_rows = load_halves(nc, keep, weight, N_GROUPS, "w")
-        x_rows = load_halves(nc, keep, x, M_GROUPS, "x")
+        starts = [sum(CHUNKS[:c]) for c in range(len(CHUNKS))]
+        w_rows = []
+        w_place = []
+        w_source = []
+        for c, width in enumerate(CHUNKS):
+            rows = weight[starts[c] : starts[c] + width, :]
+            per = width // P
+            view = rows.rearrange("(p b) k -> p b k", b=per)
+            for i in range(width // PIECE):
+                w_rows.append(keep.tile([P, 2, K], BF16, name="w%d" % len(w_rows)))
+                w_place.append((c, PIECE * i))
+                w_source.append(view[:, 2 * i : 2 * i + 2, :])
+        x_rows = [keep.tile([P, 2, K], BF16, name="x%d" % i) for i in range(M // PIECE)]
+        x_view = x.rearrange("(i b p) k -> i p b k", b=2, p=P)
         bias_all = keep.tile([P, N], BF16)
+
+        def load_w(i):
+            nc.sync.dma_start(out=w_rows[i][:], in_=w_source[i])
+
+        def load_x(i):
+            nc.sync.dma_start(out=x_rows[i][:], in_=x_view[i])
+
+        X_AFTER = 12
+        for i in range(X_AFTER):
+            load_w(i)
+        load_x(0)
+        load_x(1)
+        for i in range(X_AFTER, N_PIECES):
+            load_w(i)
+        load_x(2)
+        load_x(3)
         nc.sync.dma_start(out=bias_all[:], in_=bias.partition_broadcast(P))
 
-        w_abs = [
-            [keep.tile([P, 2, K], BF16, name="a%d_%d" % (j, h)) for h in range(2)]
-            for j in range(N_GROUPS)
+        def transpose_piece(rows, grouped, col):
+            for g in range(PASSES):
+                bank = psum.tile([P, 512], F32, tag="bank")
+                planes = bank[:].rearrange("p (u c) -> p u c", u=2)
+                for u in range(2):
+                    first = (2 * g + u) * P
+                    for b in range(2):
+                        words = rows[:, b, :].bitcast(F32)
+                        nc.tensor.transpose(
+                            planes[:, u, P * b : P * (b + 1)], words[:, first : first + P], ident[:]
+                        )
+                nc.scalar.copy(
+                    out=grouped[:, g, col : col + PIECE, :].bitcast(F32),
+                    in_=planes.rearrange("p u c -> p c u"),
+                )
+
+        w_grouped = [
+            keep.tile([P, PASSES, width, 4], BF16, name="wt%d" % c, align_bytes=64)
+            for c, width in enumerate(CHUNKS)
         ]
-        sum_scalar = keep.tile([P, N_GROUPS], F32)
-        sum_vector = keep.tile([P, N_GROUPS], F32)
-        for j in range(N_GROUPS):
-            nc.scalar.activation(
-                out=w_abs[j][0][:],
-                in_=w_rows[j][0][:],
-                func=ACT.Abs,
-                accum_out=sum_scalar[:, j : j + 1],
+        x_grouped = [
+            keep.tile([P, PASSES, X_GROUP, 4], BF16, name="xt%d" % i, align_bytes=64) for i in range(X_GROUPS)
+        ]
+        x_codes = [
+            keep.tile([P, PASSES, X_GROUP], U32, name="xc%d" % i, align_bytes=64) for i in range(X_GROUPS)
+        ]
+        x_scales = [
+            keep.tile([P, PASSES, X_GROUP], U8, name="xs%d" % i, align_bytes=64) for i in range(X_GROUPS)
+        ]
+
+        def transpose_x(i):
+            for half in range(2):
+                transpose_piece(x_rows[2 * i + half], x_grouped[i], PIECE * half)
+
+        def quantise(grouped, codes, scales):
+            nc.vector.quantize_mx(
+                out=flat(codes[:]).bitcast(FP8X4), scales=flat(scales[:]), in_=words4(grouped[:])
             )
+
+        sums = psum_s.tile([P, 512], F32, tag="sums")
+        sum_vector = keep.tile([P, N_PIECES // 2], F32)
+        tensor_pieces = [i for i in range(N_PIECES) if i % 2 == 0]
+        for i in range(N_PIECES):
+            absolute = abs_pool.tile([P, 2, K], BF16, tag="absolute")
             nc.vector.tensor_scalar(
-                out=flat(w_abs[j][1][:]).bitcast(I32),
-                in0=flat(w_rows[j][1][:]).bitcast(I32),
+                out=flat(absolute[:]).bitcast(I32),
+                in0=flat(w_rows[i][:]).bitcast(I32),
                 scalar1=ABS_BITS,
                 scalar2=None,
                 op0=ALU.bitwise_and,
             )
-            nc.vector.tensor_scalar(
-                out=flat(w_abs[j][1][:]),
-                in0=flat(w_abs[j][1][:]),
-                scalar1=0.0,
-                scalar2=None,
-                op0=ALU.max,
-                op1=ALU.add,
-                accum_out=sum_vector[:, j : j + 1],
-            )
-
-        mean_ps = psum_t.tile([P, N_GROUPS], F32, tag="tp")
-        nc.tensor.matmul(mean_ps[:], lhsT=averager[:], rhs=sum_scalar[:], start=True, stop=False)
-        nc.tensor.matmul(mean_ps[:], lhsT=averager[:], rhs=sum_vector[:], start=False, stop=True)
-        mean = keep.tile([P, 1], F32)
-        nc.vector.tensor_reduce(out=mean[:], in_=mean_ps[:], axis=mybir.AxisListType.X, op=ALU.add)
-        thr = keep.tile([P, 1], F32)
-        nc.vector.tensor_scalar(
-            out=thr[:], in0=mean[:], scalar1=EPS, scalar2=THRESHOLD, op0=ALU.max, op1=ALU.mult
-        )
-        mid = keep.tile([P, 1], F32)
-        twice_mid = keep.tile([P, 1], F32)
-        inv_twice_mid = keep.tile([P, 1], F32)
-
-        def prepare_rounding():
-            nc.vector.tensor_scalar(
-                out=mid[:].bitcast(I32),
-                in0=thr[:].bitcast(I32),
-                scalar1=TOP_BITS,
-                scalar2=MID_BIT,
-                op0=ALU.bitwise_and,
-                op1=ALU.bitwise_or,
-            )
-            nc.vector.tensor_scalar(
-                out=twice_mid[:], in0=mid[:], scalar1=2.0, scalar2=None, op0=ALU.mult
-            )
-            nc.vector.reciprocal(out=inv_twice_mid[:], in_=twice_mid[:])
-
-        def ternarise_on_vector(j, halves):
-            for h in halves:
-                compare(j, h)
-            for h in halves:
-                put_sign(j, h)
-
-        def compare(j, h):
-            nc.vector.tensor_scalar(
-                out=flat(w_abs[j][h][:]),
-                in0=flat(w_abs[j][h][:]),
-                scalar1=thr[:, 0:1],
-                scalar2=None,
-                op0=ALU.is_gt,
-            )
-
-        def put_sign(j, h):
-            nc.vector.scalar_tensor_tensor(
-                out=flat(w_rows[j][h][:]).bitcast(I32),
-                in0=flat(w_rows[j][h][:]).bitcast(I32),
-                scalar=SIGN_BITS,
-                in1=flat(w_abs[j][h][:]).bitcast(I32),
-                op0=ALU.bitwise_and,
-                op1=ALU.bitwise_or,
-            )
-
-        def ternarise_on_scalar(j, h):
-            rounded = rounded_pool.tile([P, 2, K], F32, tag="rounded")
-            nc.scalar.activation(
-                out=rounded[:],
-                in_=w_rows[j][h][:],
-                func=ACT.Copy,
-                scale=inv_twice_mid[:, 0:1],
-                bias=ROUND,
-            )
-            nc.scalar.activation(
-                out=w_rows[j][h][:], in_=rounded[:], func=ACT.Sign, bias=minus_round[:, 0:1]
-            )
-
-        def ternarise(j):
-            if j < SCALAR_FROM:
-                ternarise_on_vector(j, (1, 0))
+            chunk, col = w_place[i]
+            transpose_piece(w_rows[i], w_grouped[chunk], col)
+            if i % 2 == 0:
+                steps = 2 * K // SUM_COLS
+                for s in range(steps):
+                    nc.tensor.matmul(
+                        sums[:, 0:SUM_COLS],
+                        lhsT=averager_b[:],
+                        rhs=flat(absolute[:])[:, SUM_COLS * s : SUM_COLS * (s + 1)],
+                        start=(i == tensor_pieces[0] and s == 0),
+                        stop=(i == tensor_pieces[-1] and s == steps - 1),
+                    )
             else:
-                ternarise_on_vector(j, (1,))
-                ternarise_on_scalar(j, 0)
+                nc.vector.tensor_scalar(
+                    out=flat(absolute[:]),
+                    in0=flat(absolute[:]),
+                    scalar1=0.0,
+                    scalar2=None,
+                    op0=ALU.max,
+                    op1=ALU.add,
+                    accum_out=sum_vector[:, i // 2 : i // 2 + 1],
+                )
+            if i == X_AFTER - 1:
+                transpose_x(0)
+                quantise(x_grouped[0], x_codes[0], x_scales[0])
 
-        q_grouped = {}
+        used = SUM_COLS + N_PIECES // 2
+        nc.tensor.matmul(sums[:, SUM_COLS:used], lhsT=averager[:], rhs=sum_vector[:], start=True, stop=True)
+        mean = keep.tile([P, 1], F32)
+        nc.vector.tensor_reduce(out=mean[:], in_=sums[:, 0:used], axis=mybir.AxisListType.X, op=ALU.add)
+        half_thr = keep.tile([P, 1], F32)
+        nc.vector.tensor_scalar(
+            out=half_thr[:], in0=mean[:], scalar1=EPS, scalar2=THRESHOLD / 2, op0=ALU.max, op1=ALU.mult
+        )
+        half_edge = keep.tile([P, 1], F32)
+        nc.vector.tensor_scalar(
+            out=half_edge[:].bitcast(I32),
+            in0=half_thr[:].bitcast(I32),
+            scalar1=TOP_BITS,
+            scalar2=THREE_QUARTERS,
+            op0=ALU.bitwise_and,
+            op1=ALU.bitwise_or,
+        )
+        stretch = keep.tile([P, 1], F32)
+        nc.vector.reciprocal(out=stretch[:], in_=half_edge[:])
+
+        def stretch_on_vector(c):
+            nc.vector.tensor_scalar(
+                out=words4(w_grouped[c][:]),
+                in0=words4(w_grouped[c][:]),
+                scalar1=stretch[:, 0:1],
+                scalar2=None,
+                op0=ALU.mult,
+            )
+
+        def stretch_on_scalar(c):
+            nc.scalar.activation(
+                out=words4(w_grouped[c][:]), in_=words4(w_grouped[c][:]), func=ACT.Copy, scale=stretch[:, 0:1]
+            )
+
+        def cut(c):
+            view = words4(w_grouped[c][:]).bitcast(I32)
+            nc.vector.tensor_scalar(out=view, in0=view, scalar1=TWO_BITS, scalar2=None, op0=ALU.bitwise_and)
+
         q_codes = {}
         q_scales = {}
 
-        def transpose_q(j):
-            q_grouped[j] = transpose_group(nc, psum_t, grouped_pool, w_rows[j], ident)
+        def quantise_q(c):
+            codes = q_pool.tile([P, PASSES, CHUNKS[c]], U32, tag="codes", align_bytes=64)
+            scales = q_pool.tile([P, PASSES, CHUNKS[c]], U8, tag="scales", align_bytes=64)
+            quantise(w_grouped[c], codes, scales)
+            q_codes[c] = codes
+            q_scales[c] = scales
 
-        def quantise_q(j):
-            codes = q_pool.tile([P, PASSES, GROUP], U32, tag="codes", align_bytes=64)
-            scales = q_pool.tile([P, PASSES, GROUP], U8, tag="scales", align_bytes=64)
-            quantise_group(nc, q_grouped[j], codes, scales)
-            q_codes[j] = codes
-            q_scales[j] = scales
-
-        x_codes = [
-            keep.tile([P, PASSES, GROUP], U32, name="xc%d" % i, align_bytes=64) for i in range(M_GROUPS)
-        ]
-        x_scales = [
-            keep.tile([P, PASSES, GROUP], U8, name="xs%d" % i, align_bytes=64) for i in range(M_GROUPS)
-        ]
-
-        def multiply(j, i):
-            cols = slice(GROUP * j, GROUP * (j + 1))
-            for s in range(GROUP // P):
+        def multiply(c, i):
+            width = CHUNKS[c]
+            per = width // P
+            cols = slice(starts[c], starts[c] + width)
+            for s in range(X_GROUP // P):
                 rows = slice(P * s, P * (s + 1))
-                acc = psum_o.tile([P, GROUP], F32, tag="acc")
+                acc = psum.tile([P, 512], F32, tag="bank")
                 for g in range(PASSES):
                     nc.tensor.matmul_mx(
-                        out=acc[:],
+                        out=acc[:, 0:width],
                         lhsT=x_codes[i][:, g, rows].bitcast(FP8X4),
                         lhsT_scale=x_scales[i][:, g, rows],
-                        rhs=q_codes[j][:, g, :].bitcast(FP8X4),
-                        rhs_scale=q_scales[j][:, g, :],
+                        rhs=q_codes[c][:, g, :].bitcast(FP8X4),
+                        rhs_scale=q_scales[c][:, g, :],
                         start=(g == 0),
                         stop=(g == PASSES - 1),
                     )
-                res = res_pool.tile([P, GROUP], F32, tag="res")
-                nc.vector.tensor_tensor(out=res[:], in0=acc[:], in1=bias_all[:, cols], op=ALU.add)
-                first = GROUP * i + P * s
-                nc.sync.dma_start(out=out[first : first + P, cols], in_=res[:])
+                res = res_pool.tile([P, 512], F32, tag="res")
+                nc.vector.scalar_tensor_tensor(
+                    out=res[:, 0:width].rearrange("p (r b) -> p r b", b=per),
+                    in0=acc[:, 0:width].rearrange("p (b r) -> p r b", b=per),
+                    scalar=0.5,
+                    in1=bias_all[:, cols].rearrange("p (r b) -> p r b", b=per),
+                    op0=ALU.mult,
+                    op1=ALU.add,
+                )
+                first = X_GROUP * i + P * s
+                nc.sync.dma_start(out=out[first : first + P, cols], in_=res[:, 0:width])
 
-        ternarise(0)
-        ternarise(1)
-        prepare_rounding()
-        for i in range(M_GROUPS):
-            x_grouped = transpose_group(nc, psum_t, grouped_pool, x_rows[i], ident)
-            quantise_group(nc, x_grouped, x_codes[i], x_scales[i])
-        transpose_q(0)
+        last = len(CHUNKS) - 1
+        stretch_on_vector(0)
+        stretch_on_vector(1)
+        cut(0)
+        cut(1)
+        transpose_x(1)
+        stretch_on_scalar(2)
+        stretch_on_scalar(3)
         quantise_q(0)
-        transpose_q(1)
-        for j in range(N_GROUPS):
-            if j + 2 < N_GROUPS:
-                ternarise(j + 2)
-            multiply(j, 0)
-            if j + 1 < N_GROUPS:
-                quantise_q(j + 1)
-            multiply(j, 1)
-            if j + 2 < N_GROUPS:
-                transpose_q(j + 2)
+        quantise_q(1)
+        multiply(0, 0)
+        multiply(1, 0)
+        quantise(x_grouped[1], x_codes[1], x_scales[1])
+        multiply(0, 1)
+        cut(2)
+        multiply(1, 1)
+        quantise_q(2)
+        for c in range(2, last + 1):
+            if c + 2 <= last:
+                stretch_on_scalar(c + 2)
+            if c + 1 <= last:
+                cut(c + 1)
+            multiply(c, 0)
+            if c + 1 <= last:
+                quantise_q(c + 1)
+            multiply(c, 1)

@@ -30,6 +30,15 @@ ABS_BITS = 0x7FFF7FFF
 TWO_BITS = -0x3FFF4000
 TOP_BITS = -0x10000
 THREE_QUARTERS = 0xC000
+SCALAR_TILES = (0, 2, 4)
+TRANSPOSED_EARLY = 12
+LATE_FROM = 9
+TURNED = ()
+VECTOR_SUMS = (1, 3, 7, 9, 11)
+SCALAR_SUMS = (5,)
+MODES = "VVVMSMSMS"
+ROUND = 12582912.0
+G_PIECES = 2
 SUM_COLS = 256
 
 
@@ -45,9 +54,12 @@ def tile_bitlinear_kernel(tc, x, weight, bias, out):
     nc = tc.nc
     with ExitStack() as ctx:
         keep = ctx.enter_context(tc.tile_pool(name="keep", bufs=1))
-        abs_pool = ctx.enter_context(tc.tile_pool(name="absolute", bufs=4))
-        q_pool = ctx.enter_context(tc.tile_pool(name="q", bufs=2))
-        res_pool = ctx.enter_context(tc.tile_pool(name="res", bufs=8))
+        w_pool = ctx.enter_context(tc.tile_pool(name="w", bufs=11))
+        abs_pool = ctx.enter_context(tc.tile_pool(name="absolute", bufs=3))
+        spare_pool = ctx.enter_context(tc.tile_pool(name="spare", bufs=1))
+        round_pool = ctx.enter_context(tc.tile_pool(name="rounded", bufs=4))
+        q_pool = ctx.enter_context(tc.tile_pool(name="q", bufs=3))
+        res_pool = ctx.enter_context(tc.tile_pool(name="res", bufs=9))
         psum = ctx.enter_context(tc.psum_pool(name="psum", bufs=7))
         psum_s = ctx.enter_context(tc.psum_pool(name="psum_s", bufs=1))
         ctx.enter_context(tc.manual_schedule())
@@ -56,6 +68,8 @@ def tile_bitlinear_kernel(tc, x, weight, bias, out):
         make_identity(nc, ident[:])
         averager = keep.tile([P, P], F32)
         nc.vector.memset(averager[:], 1.0 / (N * K))
+        minus_round = keep.tile([P, 1], F32)
+        nc.vector.memset(minus_round[:], -ROUND)
         averager_b = keep.tile([P, P], BF16)
         nc.vector.memset(averager_b[:], 1.0 / (N * K))
 
@@ -68,12 +82,13 @@ def tile_bitlinear_kernel(tc, x, weight, bias, out):
             per = width // P
             view = rows.rearrange("(p b) k -> p b k", b=per)
             for i in range(width // PIECE):
-                w_rows.append(keep.tile([P, 2, K], BF16, name="w%d" % len(w_rows)))
+                w_rows.append(w_pool.tile([P, 2, K], BF16, tag="w", name="w%d" % len(w_rows)))
                 w_place.append((c, PIECE * i))
                 w_source.append(view[:, 2 * i : 2 * i + 2, :])
         x_rows = [keep.tile([P, 2, K], BF16, name="x%d" % i) for i in range(M // PIECE)]
         x_view = x.rearrange("(i b p) k -> i p b k", b=2, p=P)
         bias_all = keep.tile([P, N], BF16)
+        bias_turned = keep.tile([P, len(CHUNKS) - 2, 4], BF16)
 
         def load_w(i):
             nc.sync.dma_start(out=w_rows[i][:], in_=w_source[i])
@@ -81,18 +96,18 @@ def tile_bitlinear_kernel(tc, x, weight, bias, out):
         def load_x(i):
             nc.sync.dma_start(out=x_rows[i][:], in_=x_view[i])
 
-        X_AFTER = 12
-        for i in range(X_AFTER):
+        for i in range(N_PIECES):
             load_w(i)
         load_x(0)
         load_x(1)
-        for i in range(X_AFTER, N_PIECES):
-            load_w(i)
+        nc.sync.dma_start(out=bias_all[:], in_=bias.partition_broadcast(P))
         load_x(2)
         load_x(3)
-        nc.sync.dma_start(out=bias_all[:], in_=bias.partition_broadcast(P))
+        nc.sync.dma_start(
+            out=bias_turned[:], in_=bias[512:N].rearrange("(c p b) -> p c b", p=P, b=4)
+        )
 
-        def transpose_piece(rows, grouped, col):
+        def transpose_piece(rows, grouped, col, leave=None):
             for g in range(PASSES):
                 bank = psum.tile([P, 512], F32, tag="bank")
                 planes = bank[:].rearrange("p (u c) -> p u c", u=2)
@@ -103,10 +118,13 @@ def tile_bitlinear_kernel(tc, x, weight, bias, out):
                         nc.tensor.transpose(
                             planes[:, u, P * b : P * (b + 1)], words[:, first : first + P], ident[:]
                         )
-                nc.scalar.copy(
-                    out=grouped[:, g, col : col + PIECE, :].bitcast(F32),
-                    in_=planes.rearrange("p u c -> p c u"),
-                )
+                if leave:
+                    leave(grouped[:, g, col : col + PIECE, :], planes)
+                else:
+                    nc.scalar.copy(
+                        out=grouped[:, g, col : col + PIECE, :].bitcast(F32),
+                        in_=planes.rearrange("p u c -> p c u"),
+                    )
 
         w_grouped = [
             keep.tile([P, PASSES, width, 4], BF16, name="wt%d" % c, align_bytes=64)
@@ -132,45 +150,77 @@ def tile_bitlinear_kernel(tc, x, weight, bias, out):
             )
 
         sums = psum_s.tile([P, 512], F32, tag="sums")
-        sum_vector = keep.tile([P, N_PIECES // 2], F32)
-        tensor_pieces = [i for i in range(N_PIECES) if i % 2 == 0]
-        for i in range(N_PIECES):
+        sum_rest = keep.tile([P, N_PIECES], F32)
+        absolutes = {}
+
+        def clear_signs(i, rows):
             absolute = abs_pool.tile([P, 2, K], BF16, tag="absolute")
             nc.vector.tensor_scalar(
-                out=flat(absolute[:]).bitcast(I32),
-                in0=flat(w_rows[i][:]).bitcast(I32),
+                out=flat(absolute[:, 0:rows, :]).bitcast(I32),
+                in0=flat(w_rows[i][:, 0:rows, :]).bitcast(I32),
                 scalar1=ABS_BITS,
                 scalar2=None,
                 op0=ALU.bitwise_and,
             )
+            absolutes[i] = flat(absolute[:, 0:rows, :])
+
+        def add_on_tensor(i, first, last):
+            steps = absolutes[i].shape[1] // SUM_COLS
+            for s in range(steps):
+                nc.tensor.matmul(
+                    sums[:, 0:SUM_COLS],
+                    lhsT=averager_b[:],
+                    rhs=absolutes[i][:, SUM_COLS * s : SUM_COLS * (s + 1)],
+                    start=(first and s == 0),
+                    stop=(last and s == steps - 1),
+                )
+
+        def add_on_vector(i, column):
+            nc.vector.tensor_scalar(
+                out=absolutes[i],
+                in0=absolutes[i],
+                scalar1=0.0,
+                scalar2=None,
+                op0=ALU.max,
+                op1=ALU.add,
+                accum_out=sum_rest[:, column : column + 1],
+            )
+
+        def add_on_scalar(i, row, column):
+            spare = spare_pool.tile([P, 2, K], BF16, tag="spare")
+            nc.scalar.activation(
+                out=spare[:, row:2, :],
+                in_=w_rows[i][:, row:2, :],
+                func=ACT.Abs,
+                accum_out=sum_rest[:, column : column + 1],
+            )
+
+        def transpose_w(i):
             chunk, col = w_place[i]
             transpose_piece(w_rows[i], w_grouped[chunk], col)
-            if i % 2 == 0:
-                steps = 2 * K // SUM_COLS
-                for s in range(steps):
-                    nc.tensor.matmul(
-                        sums[:, 0:SUM_COLS],
-                        lhsT=averager_b[:],
-                        rhs=flat(absolute[:])[:, SUM_COLS * s : SUM_COLS * (s + 1)],
-                        start=(i == tensor_pieces[0] and s == 0),
-                        stop=(i == tensor_pieces[-1] and s == steps - 1),
-                    )
-            else:
-                nc.vector.tensor_scalar(
-                    out=flat(absolute[:]),
-                    in0=flat(absolute[:]),
-                    scalar1=0.0,
-                    scalar2=None,
-                    op0=ALU.max,
-                    op1=ALU.add,
-                    accum_out=sum_vector[:, i // 2 : i // 2 + 1],
-                )
-            if i == X_AFTER - 1:
-                transpose_x(0)
-                quantise(x_grouped[0], x_codes[0], x_scales[0])
 
-        used = SUM_COLS + N_PIECES // 2
-        nc.tensor.matmul(sums[:, SUM_COLS:used], lhsT=averager[:], rhs=sum_vector[:], start=True, stop=True)
+        final = N_PIECES - 1
+        rest = 0
+        for i in range(final):
+            if i not in SCALAR_SUMS:
+                clear_signs(i, 2)
+            if i < TRANSPOSED_EARLY:
+                transpose_w(i)
+            if i in SCALAR_SUMS:
+                add_on_scalar(i, 0, rest)
+                rest += 1
+            elif i in VECTOR_SUMS:
+                add_on_vector(i, rest)
+                rest += 1
+            else:
+                add_on_tensor(i, i == 0, False)
+        clear_signs(final, 1)
+        add_on_scalar(final, 1, rest)
+        rest += 1
+        add_on_tensor(final, False, True)
+
+        used = SUM_COLS + rest
+        nc.tensor.matmul(sums[:, SUM_COLS:used], lhsT=averager[:], rhs=sum_rest[:, 0:rest], start=True, stop=True)
         mean = keep.tile([P, 1], F32)
         nc.vector.tensor_reduce(out=mean[:], in_=sums[:, 0:used], axis=mybir.AxisListType.X, op=ALU.add)
         half_thr = keep.tile([P, 1], F32)
@@ -189,23 +239,81 @@ def tile_bitlinear_kernel(tc, x, weight, bias, out):
         stretch = keep.tile([P, 1], F32)
         nc.vector.reciprocal(out=stretch[:], in_=half_edge[:])
 
-        def stretch_on_vector(c):
-            nc.vector.tensor_scalar(
-                out=words4(w_grouped[c][:]),
-                in0=words4(w_grouped[c][:]),
-                scalar1=stretch[:, 0:1],
-                scalar2=None,
-                op0=ALU.mult,
-            )
+        def quarters(c, first, count):
+            view = words4(w_grouped[c][:])
+            size = view.shape[1] // 4
+            return view[:, size * first : size * (first + count)]
 
-        def stretch_on_scalar(c):
-            nc.scalar.activation(
-                out=words4(w_grouped[c][:]), in_=words4(w_grouped[c][:]), func=ACT.Copy, scale=stretch[:, 0:1]
-            )
+        def stretch_on_vector(c, first=0, count=4):
+            view = quarters(c, first, count)
+            nc.vector.tensor_scalar(out=view, in0=view, scalar1=stretch[:, 0:1], scalar2=None, op0=ALU.mult)
+
+        def stretch_on_scalar(c, first, count=1):
+            view = quarters(c, first, count)
+            nc.scalar.activation(out=view, in_=view, func=ACT.Copy, scale=stretch[:, 0:1])
 
         def cut(c):
             view = words4(w_grouped[c][:]).bitcast(I32)
             nc.vector.tensor_scalar(out=view, in0=view, scalar1=TWO_BITS, scalar2=None, op0=ALU.bitwise_and)
+
+        rounding = keep.tile([P, 1], F32)
+        nc.vector.tensor_scalar(
+            out=rounding[:], in0=stretch[:], scalar1=0.25, scalar2=None, op0=ALU.mult
+        )
+        rounded = {}
+
+        def round_on_scalar(c, part):
+            rounded[c, part] = round_pool.tile([P, 1024], F32, tag="rounded", name="rounded%d_%d" % (c, part))
+            nc.scalar.activation(
+                out=rounded[c, part][:],
+                in_=quarters(c, part, 1),
+                func=ACT.Copy,
+                scale=rounding[:, 0:1],
+                bias=ROUND,
+            )
+
+        def round_on_gpsimd(c, part):
+            rounded[c, part] = round_pool.tile([P, 1024], F32, tag="rounded", name="rounded%d_%d" % (c, part))
+            for n in range(G_PIECES):
+                size = 1024 // G_PIECES
+                cols = slice(size * n, size * (n + 1))
+                nc.gpsimd.tensor_scalar(
+                    out=rounded[c, part][:, cols],
+                    in0=quarters(c, part, 1)[:, cols],
+                    scalar1=rounding[:, 0:1],
+                    scalar2=ROUND,
+                    op0=ALU.mult,
+                    op1=ALU.add,
+                )
+
+        def sign_on_scalar(c, part):
+            nc.scalar.activation(
+                out=quarters(c, part, 1), in_=rounded[c, part][:], func=ACT.Sign, bias=minus_round[:, 0:1]
+            )
+
+        def leave_rounded(out, planes):
+            tile = round_pool.tile([P, 1024], F32, tag="rounded")
+            nc.scalar.activation(
+                out=tile[:].rearrange("p (c u e) -> p c u e", u=2, e=2),
+                in_=planes.bitcast(BF16).rearrange("p u (c e) -> p c u e", e=2),
+                func=ACT.Copy,
+                scale=rounding[:, 0:1],
+                bias=ROUND,
+            )
+            nc.scalar.activation(
+                out=out.rearrange("p c t -> p (c t)"), in_=tile[:], func=ACT.Sign, bias=minus_round[:, 0:1]
+            )
+
+        def scalar_jobs(c):
+            if MODES[c] == "M":
+                return [(stretch_on_scalar, c, part) for part in range(3)]
+            if MODES[c] == "C":
+                return [(job, c, part) for part in range(4) for job in (round_on_gpsimd, sign_on_scalar)]
+            if MODES[c] == "S" and c < LATE_FROM:
+                return [
+                    (job, c, part) for pair in ((0, 1), (2, 3)) for job in (round_on_scalar, sign_on_scalar) for part in pair
+                ]
+            return []
 
         q_codes = {}
         q_scales = {}
@@ -217,58 +325,156 @@ def tile_bitlinear_kernel(tc, x, weight, bias, out):
             q_codes[c] = codes
             q_scales[c] = scales
 
-        def multiply(c, i):
+        def multiply(c, m, on_scalar):
             width = CHUNKS[c]
             per = width // P
             cols = slice(starts[c], starts[c] + width)
-            for s in range(X_GROUP // P):
-                rows = slice(P * s, P * (s + 1))
-                acc = psum.tile([P, 512], F32, tag="bank")
-                for g in range(PASSES):
-                    nc.tensor.matmul_mx(
-                        out=acc[:, 0:width],
-                        lhsT=x_codes[i][:, g, rows].bitcast(FP8X4),
-                        lhsT_scale=x_scales[i][:, g, rows],
-                        rhs=q_codes[c][:, g, :].bitcast(FP8X4),
-                        rhs_scale=q_scales[c][:, g, :],
-                        start=(g == 0),
-                        stop=(g == PASSES - 1),
-                    )
-                res = res_pool.tile([P, 512], F32, tag="res")
+            i = m * P // X_GROUP
+            rows = slice(m * P - i * X_GROUP, m * P - i * X_GROUP + P)
+            acc = psum.tile([P, 512], F32, tag="bank")
+            for g in range(PASSES):
+                nc.tensor.matmul_mx(
+                    out=acc[:, 0:width],
+                    lhsT=x_codes[i][:, g, rows].bitcast(FP8X4),
+                    lhsT_scale=x_scales[i][:, g, rows],
+                    rhs=q_codes[c][:, g, :].bitcast(FP8X4),
+                    rhs_scale=q_scales[c][:, g, :],
+                    start=(g == 0),
+                    stop=(g == PASSES - 1),
+                )
+            res = res_pool.tile([P, 512], F32, tag="res")
+            in_order = acc[:, 0:width].rearrange("p (b r) -> p r b", b=per)
+            result = res[:, 0:width].rearrange("p (r b) -> p r b", b=per)
+            factor = 0.5 if MODES[c] in "MV" else 1.0
+            if on_scalar:
+                nc.scalar.activation(out=result, in_=in_order, func=ACT.Copy, scale=factor)
+                nc.gpsimd.tensor_tensor(
+                    out=res[:, 0:width], in0=res[:, 0:width], in1=bias_all[:, cols], op=ALU.add
+                )
+            else:
                 nc.vector.scalar_tensor_tensor(
-                    out=res[:, 0:width].rearrange("p (r b) -> p r b", b=per),
-                    in0=acc[:, 0:width].rearrange("p (b r) -> p r b", b=per),
-                    scalar=0.5,
+                    out=result,
+                    in0=in_order,
+                    scalar=factor,
                     in1=bias_all[:, cols].rearrange("p (r b) -> p r b", b=per),
                     op0=ALU.mult,
                     op1=ALU.add,
                 )
-                first = X_GROUP * i + P * s
-                nc.sync.dma_start(out=out[first : first + P, cols], in_=res[:, 0:width])
+            nc.sync.dma_start(out=out[P * m : P * (m + 1), cols], in_=res[:, 0:width])
+
+        turned_pool = ctx.enter_context(tc.tile_pool(name="turned", bufs=4))
+
+        def multiply_turned(c, i):
+            factor = 0.5 if MODES[c] in "MV" else 1.0
+            turned = []
+            for b in range(4):
+                some = slice(P * b, P * (b + 1))
+                acc = psum.tile([P, 512], F32, tag="bank")
+                for g in range(PASSES):
+                    nc.tensor.matmul_mx(
+                        out=acc[:],
+                        lhsT=q_codes[c][:, g, some].bitcast(FP8X4),
+                        lhsT_scale=q_scales[c][:, g, some],
+                        rhs=x_codes[i][:, g, :].bitcast(FP8X4),
+                        rhs_scale=x_scales[i][:, g, :],
+                        start=(g == 0),
+                        stop=(g == PASSES - 1),
+                    )
+                tile = turned_pool.tile([P, 512], F32, tag="turned", name="turned%d_%d_%d" % (c, i, b))
+                nc.scalar.activation(
+                    out=tile[:],
+                    in_=acc[:],
+                    func=ACT.Identity,
+                    scale=factor,
+                    bias=bias_turned[:, c - 2, b : b + 1],
+                )
+                turned.append(tile)
+            return turned
+
+        def turn_back(c, i, turned, s):
+            cols = slice(starts[c], starts[c] + 512)
+            bank = psum.tile([P, 512], F32, tag="bank")
+            for b in range(4):
+                nc.tensor.transpose(
+                    bank[:, P * b : P * (b + 1)], turned[b][:, P * s : P * (s + 1)], ident[:]
+                )
+            res = res_pool.tile([P, 512], F32, tag="res")
+            nc.scalar.copy(
+                out=res[:].rearrange("p (r b) -> p r b", b=4), in_=bank[:].rearrange("p (b r) -> p r b", b=4)
+            )
+            first = X_GROUP * i + P * s
+            nc.sync.dma_start(out=out[first : first + P, cols], in_=res[:])
 
         last = len(CHUNKS) - 1
-        stretch_on_vector(0)
-        stretch_on_vector(1)
-        cut(0)
-        cut(1)
-        transpose_x(1)
-        stretch_on_scalar(2)
-        stretch_on_scalar(3)
-        quantise_q(0)
-        quantise_q(1)
-        multiply(0, 0)
-        multiply(1, 0)
-        quantise(x_grouped[1], x_codes[1], x_scales[1])
-        multiply(0, 1)
+        per_group = X_GROUP // P
+        m_tiles = M // P
+        late = list(range(TRANSPOSED_EARLY, N_PIECES))
+
+        def prepare(c):
+            for job, chunk, part in scalar_jobs(c):
+                job(chunk, part)
+
+        def vector_share(c):
+            if MODES[c] == "V":
+                stretch_on_vector(c)
+            if MODES[c] == "M":
+                stretch_on_vector(c, 3, 1)
+
+        def vector_cut(c):
+            if MODES[c] in "MV":
+                cut(c)
+
+        def late_piece():
+            i = late.pop(0)
+            chunk, col = w_place[i]
+            transpose_piece(w_rows[i], w_grouped[chunk], col, leave_rounded)
+
+        def late_piece():
+            i = late.pop(0)
+            transpose_w(i)
+
+        for c in (0, 1):
+            stretch_on_vector(c)
+        for c in (0, 1):
+            cut(c)
+        transpose_x(0)
+        for c in (0, 1):
+            quantise_q(c)
+        for n in range(len(late) // 2):
+            late_piece()
+        quantise(x_grouped[0], x_codes[0], x_scales[0])
+        stretch_on_vector(2)
+        for m in range(per_group):
+            multiply(0, m, False)
         cut(2)
-        multiply(1, 1)
+        transpose_x(1)
+        prepare(3)
+        vector_share(3)
+        for m in range(per_group):
+            multiply(1, m, False)
+        while late:
+            late_piece()
         quantise_q(2)
+        quantise(x_grouped[1], x_codes[1], x_scales[1])
+        prepare(4)
+        for m in range(per_group, m_tiles):
+            multiply(0, m, False)
+        vector_cut(3)
+        for m in range(per_group, m_tiles):
+            multiply(1, m, False)
         for c in range(2, last + 1):
-            if c + 2 <= last:
-                stretch_on_scalar(c + 2)
-            if c + 1 <= last:
-                cut(c + 1)
-            multiply(c, 0)
-            if c + 1 <= last:
-                quantise_q(c + 1)
-            multiply(c, 1)
+            if c + 3 <= last:
+                prepare(c + 3)
+            if c in TURNED:
+                turned = multiply_turned(c, 1)
+            for m in range(m_tiles):
+                if c in TURNED and m >= per_group:
+                    turn_back(c, 1, turned, m - per_group)
+                else:
+                    multiply(c, m, c == last and m in SCALAR_TILES)
+                if m == 2 and c + 1 <= last:
+                    quantise_q(c + 1)
+                if m == 4 and c + 2 <= last:
+                    vector_share(c + 2)
+                if m == 6 and c + 2 <= last:
+                    vector_cut(c + 2)

@@ -30,15 +30,12 @@ ABS_BITS = 0x7FFF7FFF
 TWO_BITS = -0x3FFF4000
 TOP_BITS = -0x10000
 THREE_QUARTERS = 0xC000
-SCALAR_TILES = (0, 2, 4)
+SCALAR_TILES = (5, 6)
+BATCH_AT = 1
 TRANSPOSED_EARLY = 12
-LATE_FROM = 9
-TURNED = ()
 VECTOR_SUMS = (1, 3, 7, 9, 11)
 SCALAR_SUMS = (5,)
-MODES = "VVVMSMSMS"
-ROUND = 12582912.0
-G_PIECES = 2
+JOB_TILES = 6
 SUM_COLS = 256
 
 
@@ -57,9 +54,8 @@ def tile_bitlinear_kernel(tc, x, weight, bias, out):
         w_pool = ctx.enter_context(tc.tile_pool(name="w", bufs=11))
         abs_pool = ctx.enter_context(tc.tile_pool(name="absolute", bufs=3))
         spare_pool = ctx.enter_context(tc.tile_pool(name="spare", bufs=1))
-        round_pool = ctx.enter_context(tc.tile_pool(name="rounded", bufs=4))
         q_pool = ctx.enter_context(tc.tile_pool(name="q", bufs=3))
-        res_pool = ctx.enter_context(tc.tile_pool(name="res", bufs=9))
+        res_pool = ctx.enter_context(tc.tile_pool(name="res", bufs=16))
         psum = ctx.enter_context(tc.psum_pool(name="psum", bufs=7))
         psum_s = ctx.enter_context(tc.psum_pool(name="psum_s", bufs=1))
         ctx.enter_context(tc.manual_schedule())
@@ -68,8 +64,6 @@ def tile_bitlinear_kernel(tc, x, weight, bias, out):
         make_identity(nc, ident[:])
         averager = keep.tile([P, P], F32)
         nc.vector.memset(averager[:], 1.0 / (N * K))
-        minus_round = keep.tile([P, 1], F32)
-        nc.vector.memset(minus_round[:], -ROUND)
         averager_b = keep.tile([P, P], BF16)
         nc.vector.memset(averager_b[:], 1.0 / (N * K))
 
@@ -88,7 +82,6 @@ def tile_bitlinear_kernel(tc, x, weight, bias, out):
         x_rows = [keep.tile([P, 2, K], BF16, name="x%d" % i) for i in range(M // PIECE)]
         x_view = x.rearrange("(i b p) k -> i p b k", b=2, p=P)
         bias_all = keep.tile([P, N], BF16)
-        bias_turned = keep.tile([P, len(CHUNKS) - 2, 4], BF16)
 
         def load_w(i):
             nc.sync.dma_start(out=w_rows[i][:], in_=w_source[i])
@@ -103,11 +96,8 @@ def tile_bitlinear_kernel(tc, x, weight, bias, out):
         nc.sync.dma_start(out=bias_all[:], in_=bias.partition_broadcast(P))
         load_x(2)
         load_x(3)
-        nc.sync.dma_start(
-            out=bias_turned[:], in_=bias[512:N].rearrange("(c p b) -> p c b", p=P, b=4)
-        )
 
-        def transpose_piece(rows, grouped, col, leave=None):
+        def transpose_piece(rows, grouped, col):
             for g in range(PASSES):
                 bank = psum.tile([P, 512], F32, tag="bank")
                 planes = bank[:].rearrange("p (u c) -> p u c", u=2)
@@ -118,13 +108,10 @@ def tile_bitlinear_kernel(tc, x, weight, bias, out):
                         nc.tensor.transpose(
                             planes[:, u, P * b : P * (b + 1)], words[:, first : first + P], ident[:]
                         )
-                if leave:
-                    leave(grouped[:, g, col : col + PIECE, :], planes)
-                else:
-                    nc.scalar.copy(
-                        out=grouped[:, g, col : col + PIECE, :].bitcast(F32),
-                        in_=planes.rearrange("p u c -> p c u"),
-                    )
+                nc.scalar.copy(
+                    out=grouped[:, g, col : col + PIECE, :].bitcast(F32),
+                    in_=planes.rearrange("p u c -> p c u"),
+                )
 
         w_grouped = [
             keep.tile([P, PASSES, width, 4], BF16, name="wt%d" % c, align_bytes=64)
@@ -256,65 +243,6 @@ def tile_bitlinear_kernel(tc, x, weight, bias, out):
             view = words4(w_grouped[c][:]).bitcast(I32)
             nc.vector.tensor_scalar(out=view, in0=view, scalar1=TWO_BITS, scalar2=None, op0=ALU.bitwise_and)
 
-        rounding = keep.tile([P, 1], F32)
-        nc.vector.tensor_scalar(
-            out=rounding[:], in0=stretch[:], scalar1=0.25, scalar2=None, op0=ALU.mult
-        )
-        rounded = {}
-
-        def round_on_scalar(c, part):
-            rounded[c, part] = round_pool.tile([P, 1024], F32, tag="rounded", name="rounded%d_%d" % (c, part))
-            nc.scalar.activation(
-                out=rounded[c, part][:],
-                in_=quarters(c, part, 1),
-                func=ACT.Copy,
-                scale=rounding[:, 0:1],
-                bias=ROUND,
-            )
-
-        def round_on_gpsimd(c, part):
-            rounded[c, part] = round_pool.tile([P, 1024], F32, tag="rounded", name="rounded%d_%d" % (c, part))
-            for n in range(G_PIECES):
-                size = 1024 // G_PIECES
-                cols = slice(size * n, size * (n + 1))
-                nc.gpsimd.tensor_scalar(
-                    out=rounded[c, part][:, cols],
-                    in0=quarters(c, part, 1)[:, cols],
-                    scalar1=rounding[:, 0:1],
-                    scalar2=ROUND,
-                    op0=ALU.mult,
-                    op1=ALU.add,
-                )
-
-        def sign_on_scalar(c, part):
-            nc.scalar.activation(
-                out=quarters(c, part, 1), in_=rounded[c, part][:], func=ACT.Sign, bias=minus_round[:, 0:1]
-            )
-
-        def leave_rounded(out, planes):
-            tile = round_pool.tile([P, 1024], F32, tag="rounded")
-            nc.scalar.activation(
-                out=tile[:].rearrange("p (c u e) -> p c u e", u=2, e=2),
-                in_=planes.bitcast(BF16).rearrange("p u (c e) -> p c u e", e=2),
-                func=ACT.Copy,
-                scale=rounding[:, 0:1],
-                bias=ROUND,
-            )
-            nc.scalar.activation(
-                out=out.rearrange("p c t -> p (c t)"), in_=tile[:], func=ACT.Sign, bias=minus_round[:, 0:1]
-            )
-
-        def scalar_jobs(c):
-            if MODES[c] == "M":
-                return [(stretch_on_scalar, c, part) for part in range(3)]
-            if MODES[c] == "C":
-                return [(job, c, part) for part in range(4) for job in (round_on_gpsimd, sign_on_scalar)]
-            if MODES[c] == "S" and c < LATE_FROM:
-                return [
-                    (job, c, part) for pair in ((0, 1), (2, 3)) for job in (round_on_scalar, sign_on_scalar) for part in pair
-                ]
-            return []
-
         q_codes = {}
         q_scales = {}
 
@@ -345,9 +273,8 @@ def tile_bitlinear_kernel(tc, x, weight, bias, out):
             res = res_pool.tile([P, 512], F32, tag="res")
             in_order = acc[:, 0:width].rearrange("p (b r) -> p r b", b=per)
             result = res[:, 0:width].rearrange("p (r b) -> p r b", b=per)
-            factor = 0.5 if MODES[c] in "MV" else 1.0
             if on_scalar:
-                nc.scalar.activation(out=result, in_=in_order, func=ACT.Copy, scale=factor)
+                nc.scalar.activation(out=result, in_=in_order, func=ACT.Copy, scale=0.5)
                 nc.gpsimd.tensor_tensor(
                     out=res[:, 0:width], in0=res[:, 0:width], in1=bias_all[:, cols], op=ALU.add
                 )
@@ -355,83 +282,21 @@ def tile_bitlinear_kernel(tc, x, weight, bias, out):
                 nc.vector.scalar_tensor_tensor(
                     out=result,
                     in0=in_order,
-                    scalar=factor,
+                    scalar=0.5,
                     in1=bias_all[:, cols].rearrange("p (r b) -> p r b", b=per),
                     op0=ALU.mult,
                     op1=ALU.add,
                 )
             nc.sync.dma_start(out=out[P * m : P * (m + 1), cols], in_=res[:, 0:width])
 
-        turned_pool = ctx.enter_context(tc.tile_pool(name="turned", bufs=4))
-
-        def multiply_turned(c, i):
-            factor = 0.5 if MODES[c] in "MV" else 1.0
-            turned = []
-            for b in range(4):
-                some = slice(P * b, P * (b + 1))
-                acc = psum.tile([P, 512], F32, tag="bank")
-                for g in range(PASSES):
-                    nc.tensor.matmul_mx(
-                        out=acc[:],
-                        lhsT=q_codes[c][:, g, some].bitcast(FP8X4),
-                        lhsT_scale=q_scales[c][:, g, some],
-                        rhs=x_codes[i][:, g, :].bitcast(FP8X4),
-                        rhs_scale=x_scales[i][:, g, :],
-                        start=(g == 0),
-                        stop=(g == PASSES - 1),
-                    )
-                tile = turned_pool.tile([P, 512], F32, tag="turned", name="turned%d_%d_%d" % (c, i, b))
-                nc.scalar.activation(
-                    out=tile[:],
-                    in_=acc[:],
-                    func=ACT.Identity,
-                    scale=factor,
-                    bias=bias_turned[:, c - 2, b : b + 1],
-                )
-                turned.append(tile)
-            return turned
-
-        def turn_back(c, i, turned, s):
-            cols = slice(starts[c], starts[c] + 512)
-            bank = psum.tile([P, 512], F32, tag="bank")
-            for b in range(4):
-                nc.tensor.transpose(
-                    bank[:, P * b : P * (b + 1)], turned[b][:, P * s : P * (s + 1)], ident[:]
-                )
-            res = res_pool.tile([P, 512], F32, tag="res")
-            nc.scalar.copy(
-                out=res[:].rearrange("p (r b) -> p r b", b=4), in_=bank[:].rearrange("p (b r) -> p r b", b=4)
-            )
-            first = X_GROUP * i + P * s
-            nc.sync.dma_start(out=out[first : first + P, cols], in_=res[:])
-
         last = len(CHUNKS) - 1
         per_group = X_GROUP // P
         m_tiles = M // P
         late = list(range(TRANSPOSED_EARLY, N_PIECES))
 
-        def prepare(c):
-            for job, chunk, part in scalar_jobs(c):
-                job(chunk, part)
-
-        def vector_share(c):
-            if MODES[c] == "V":
-                stretch_on_vector(c)
-            if MODES[c] == "M":
-                stretch_on_vector(c, 3, 1)
-
-        def vector_cut(c):
-            if MODES[c] in "MV":
-                cut(c)
-
-        def late_piece():
-            i = late.pop(0)
-            chunk, col = w_place[i]
-            transpose_piece(w_rows[i], w_grouped[chunk], col, leave_rounded)
-
-        def late_piece():
-            i = late.pop(0)
-            transpose_w(i)
+        def transpose_late(count):
+            for n in range(count):
+                transpose_w(late.pop(0))
 
         for c in (0, 1):
             stretch_on_vector(c)
@@ -440,41 +305,34 @@ def tile_bitlinear_kernel(tc, x, weight, bias, out):
         transpose_x(0)
         for c in (0, 1):
             quantise_q(c)
-        for n in range(len(late) // 2):
-            late_piece()
+        transpose_late(2)
         quantise(x_grouped[0], x_codes[0], x_scales[0])
         stretch_on_vector(2)
         for m in range(per_group):
             multiply(0, m, False)
         cut(2)
         transpose_x(1)
-        prepare(3)
-        vector_share(3)
+        stretch_on_vector(3)
         for m in range(per_group):
             multiply(1, m, False)
-        while late:
-            late_piece()
+        transpose_late(2)
         quantise_q(2)
         quantise(x_grouped[1], x_codes[1], x_scales[1])
-        prepare(4)
+        for part in range(4):
+            stretch_on_scalar(4, part)
         for m in range(per_group, m_tiles):
             multiply(0, m, False)
-        vector_cut(3)
+        cut(3)
         for m in range(per_group, m_tiles):
             multiply(1, m, False)
         for c in range(2, last + 1):
-            if c + 3 <= last:
-                prepare(c + 3)
-            if c in TURNED:
-                turned = multiply_turned(c, 1)
+            parts = list(range(4)) if c + 3 <= last else []
             for m in range(m_tiles):
-                if c in TURNED and m >= per_group:
-                    turn_back(c, 1, turned, m - per_group)
-                else:
-                    multiply(c, m, c == last and m in SCALAR_TILES)
-                if m == 2 and c + 1 <= last:
-                    quantise_q(c + 1)
-                if m == 4 and c + 2 <= last:
-                    vector_share(c + 2)
-                if m == 6 and c + 2 <= last:
-                    vector_cut(c + 2)
+                while parts and parts[0] <= 4 * m // JOB_TILES:
+                    stretch_on_scalar(c + 3, parts.pop(0))
+                multiply(c, m, m in SCALAR_TILES)
+                if m == BATCH_AT:
+                    if c + 2 <= last:
+                        cut(c + 2)
+                    if c + 1 <= last:
+                        quantise_q(c + 1)

@@ -23,19 +23,24 @@ PIECE = 2 * P
 PASSES = K // 512
 X_GROUP = 512
 X_GROUPS = M // X_GROUP
-CHUNKS = [256, 256, 512, 512, 512, 512, 512, 512, 512]
+CHUNKS = [256, 256, 512, 512, 512, 512, 512, 512, 256, 256]
 N_PIECES = N // PIECE
 
 ABS_BITS = 0x7FFF7FFF
 TWO_BITS = -0x3FFF4000
 TOP_BITS = -0x10000
 THREE_QUARTERS = 0xC000
-SCALAR_TILES = (5, 6)
-BATCH_AT = 1
-TRANSPOSED_EARLY = 12
-VECTOR_SUMS = (1, 3, 7, 9, 11)
-SCALAR_SUMS = (5,)
-JOB_TILES = 6
+SCALAR_TILES = ((), (), (2, 5), (2, 5), (2, 5), (2, 5), (2, 5), (2, 5), (), ())
+TRANSPOSED_EARLY = 10
+VECTOR_SUMS = (1, 3, 5, 7, 9, 11)
+SCALAR_SUMS = (2, 12)
+JOB_TILES = 8
+JOB_FIRST = 0
+STORE_LAG = 2
+FINISH_AT = 0
+CUT_AT = 1
+SHARES = (0, 0, 0, 4, 4, 4, 4, 4, 4, 4)
+QUANTISE_AT = 4
 SUM_COLS = 256
 
 
@@ -54,7 +59,7 @@ def tile_bitlinear_kernel(tc, x, weight, bias, out):
         w_pool = ctx.enter_context(tc.tile_pool(name="w", bufs=11))
         abs_pool = ctx.enter_context(tc.tile_pool(name="absolute", bufs=3))
         spare_pool = ctx.enter_context(tc.tile_pool(name="spare", bufs=1))
-        q_pool = ctx.enter_context(tc.tile_pool(name="q", bufs=3))
+        q_pool = ctx.enter_context(tc.tile_pool(name="q", bufs=4))
         res_pool = ctx.enter_context(tc.tile_pool(name="res", bufs=16))
         psum = ctx.enter_context(tc.psum_pool(name="psum", bufs=7))
         psum_s = ctx.enter_context(tc.psum_pool(name="psum_s", bufs=1))
@@ -97,7 +102,7 @@ def tile_bitlinear_kernel(tc, x, weight, bias, out):
         load_x(2)
         load_x(3)
 
-        def transpose_piece(rows, grouped, col):
+        def transpose_piece(rows, grouped, col, leave):
             for g in range(PASSES):
                 bank = psum.tile([P, 512], F32, tag="bank")
                 planes = bank[:].rearrange("p (u c) -> p u c", u=2)
@@ -108,10 +113,10 @@ def tile_bitlinear_kernel(tc, x, weight, bias, out):
                         nc.tensor.transpose(
                             planes[:, u, P * b : P * (b + 1)], words[:, first : first + P], ident[:]
                         )
-                nc.scalar.copy(
-                    out=grouped[:, g, col : col + PIECE, :].bitcast(F32),
-                    in_=planes.rearrange("p u c -> p c u"),
-                )
+                leave(grouped[:, g, col : col + PIECE, :], planes)
+
+        def leave_unchanged(out, planes):
+            nc.scalar.copy(out=out.bitcast(F32), in_=planes.rearrange("p u c -> p c u"))
 
         w_grouped = [
             keep.tile([P, PASSES, width, 4], BF16, name="wt%d" % c, align_bytes=64)
@@ -129,7 +134,7 @@ def tile_bitlinear_kernel(tc, x, weight, bias, out):
 
         def transpose_x(i):
             for half in range(2):
-                transpose_piece(x_rows[2 * i + half], x_grouped[i], PIECE * half)
+                transpose_piece(x_rows[2 * i + half], x_grouped[i], PIECE * half, leave_unchanged)
 
         def quantise(grouped, codes, scales):
             nc.vector.quantize_mx(
@@ -182,9 +187,9 @@ def tile_bitlinear_kernel(tc, x, weight, bias, out):
                 accum_out=sum_rest[:, column : column + 1],
             )
 
-        def transpose_w(i):
+        def transpose_w(i, leave):
             chunk, col = w_place[i]
-            transpose_piece(w_rows[i], w_grouped[chunk], col)
+            transpose_piece(w_rows[i], w_grouped[chunk], col, leave)
 
         final = N_PIECES - 1
         rest = 0
@@ -192,7 +197,7 @@ def tile_bitlinear_kernel(tc, x, weight, bias, out):
             if i not in SCALAR_SUMS:
                 clear_signs(i, 2)
             if i < TRANSPOSED_EARLY:
-                transpose_w(i)
+                transpose_w(i, leave_unchanged)
             if i in SCALAR_SUMS:
                 add_on_scalar(i, 0, rest)
                 rest += 1
@@ -287,52 +292,85 @@ def tile_bitlinear_kernel(tc, x, weight, bias, out):
                     op0=ALU.mult,
                     op1=ALU.add,
                 )
-            nc.sync.dma_start(out=out[P * m : P * (m + 1), cols], in_=res[:, 0:width])
+            stores.append((STORE_LAG if on_scalar else 0, out[P * m : P * (m + 1), cols], res[:, 0:width]))
+            flush(1)
+
+        stores = []
+
+        def flush(age):
+            waiting = [(lag - age, place, result) for lag, place, result in stores if lag > 0]
+            for lag, place, result in stores:
+                if lag <= 0:
+                    nc.sync.dma_start(out=place, in_=result)
+            stores.clear()
+            stores.extend(waiting)
 
         last = len(CHUNKS) - 1
         per_group = X_GROUP // P
         m_tiles = M // P
         late = list(range(TRANSPOSED_EARLY, N_PIECES))
 
-        def transpose_late(count):
-            for n in range(count):
-                transpose_w(late.pop(0))
+        def leave_stretched(out, planes):
+            nc.scalar.activation(
+                out=out.rearrange("p c (u e) -> p c u e", u=2),
+                in_=planes.bitcast(BF16).rearrange("p u (c e) -> p c u e", e=2),
+                func=ACT.Copy,
+                scale=stretch[:, 0:1],
+            )
 
+        def scalar_jobs(c):
+            pieces = [i for i in late if w_place[i][0] == c]
+            if pieces:
+                return [(transpose_w, i, leave_stretched) for i in pieces]
+            return [(stretch_on_scalar, c, part) for part in range(SHARES[c])]
+
+        def stretch_chunk(c):
+            for job, one, two in scalar_jobs(c):
+                job(one, two)
+
+        def finish_chunk(c):
+            if SHARES[c] < 4:
+                stretch_on_vector(c, SHARES[c], 4 - SHARES[c])
+
+        early, later = range(per_group), range(per_group, m_tiles)
         for c in (0, 1):
             stretch_on_vector(c)
         for c in (0, 1):
             cut(c)
         transpose_x(0)
+        transpose_x(1)
         for c in (0, 1):
             quantise_q(c)
-        transpose_late(2)
         quantise(x_grouped[0], x_codes[0], x_scales[0])
-        stretch_on_vector(2)
-        for m in range(per_group):
+        stretch_chunk(2)
+        finish_chunk(2)
+        for m in early:
             multiply(0, m, False)
-        cut(2)
-        transpose_x(1)
-        stretch_on_vector(3)
-        for m in range(per_group):
-            multiply(1, m, False)
-        transpose_late(2)
-        quantise_q(2)
         quantise(x_grouped[1], x_codes[1], x_scales[1])
-        for part in range(4):
-            stretch_on_scalar(4, part)
-        for m in range(per_group, m_tiles):
-            multiply(0, m, False)
-        cut(3)
-        for m in range(per_group, m_tiles):
+        for m in early:
             multiply(1, m, False)
+        stretch_chunk(3)
+        cut(2)
+        for m in later:
+            multiply(0, m, False)
+        quantise_q(2)
+        for m in later:
+            multiply(1, m, False)
+        stretch_chunk(4)
         for c in range(2, last + 1):
-            parts = list(range(4)) if c + 3 <= last else []
+            jobs = scalar_jobs(c + 3) if c + 3 <= last else []
+            step = JOB_TILES // max(1, len(jobs))
             for m in range(m_tiles):
-                while parts and parts[0] <= 4 * m // JOB_TILES:
-                    stretch_on_scalar(c + 3, parts.pop(0))
-                multiply(c, m, m in SCALAR_TILES)
-                if m == BATCH_AT:
-                    if c + 2 <= last:
-                        cut(c + 2)
-                    if c + 1 <= last:
-                        quantise_q(c + 1)
+                if jobs and m % step == JOB_FIRST:
+                    job, one, two = jobs.pop(0)
+                    job(one, two)
+                multiply(c, m, m in SCALAR_TILES[c])
+                if m == FINISH_AT and c + 1 <= last:
+                    finish_chunk(c + 1)
+                if m == CUT_AT and c + 1 <= last:
+                    cut(c + 1)
+                if m == QUANTISE_AT and c + 1 <= last:
+                    quantise_q(c + 1)
+        flush(1)
+        while stores:
+            flush(1)

@@ -30,15 +30,15 @@ ABS_BITS = 0x7FFF7FFF
 TWO_BITS = -0x3FFF4000
 TOP_BITS = -0x10000
 THREE_QUARTERS = 0xC000
-SCALAR_TILES = ((), (), (2, 5), (2, 5), (2, 5), (2, 5), (2, 5), (2, 5), (), ())
+SCALAR_TILES = ((), (), (0, 4), (0, 4), (0, 4), (0, 4), (0, 4), (0, 4), (), ())
 TRANSPOSED_EARLY = 10
-VECTOR_SUMS = (1, 3, 5, 7, 9, 11)
+VECTOR_SUMS = (1, 4, 6, 8, 10)
 SCALAR_SUMS = (2, 12)
 JOB_TILES = 8
-JOB_FIRST = 0
+JOB_FIRST = 1
 STORE_LAG = 2
 FINISH_AT = 0
-CUT_AT = 1
+CUT_AT = 0
 SHARES = (0, 0, 0, 4, 4, 4, 4, 4, 4, 4)
 QUANTISE_AT = 4
 SUM_COLS = 256

from contextlib import ExitStack

import concourse.mybir as mybir
from concourse.masks import make_identity

F32 = mybir.dt.float32
BF16 = mybir.dt.bfloat16
I32 = mybir.dt.int32
U32 = mybir.dt.uint32
U8 = mybir.dt.uint8
FP8X4 = mybir.dt.float8_e4m3fn_x4
ALU = mybir.AluOpType
ACT = mybir.ActivationFunctionType

P = 128
M, K, N = 1024, 1024, 4096
FLOPS = 2 * M * K * N

THRESHOLD = 0.05
EPS = 1e-6

PIECE = 2 * P
PASSES = K // 512
X_GROUP = 512
X_GROUPS = M // X_GROUP
CHUNKS = [256, 256, 512, 512, 512, 512, 512, 512, 256, 256]
N_PIECES = N // PIECE

ABS_BITS = 0x7FFF7FFF
TWO_BITS = -0x3FFF4000
TOP_BITS = -0x10000
THREE_QUARTERS = 0xC000
SCALAR_TILES = ((), (), (0, 4), (0, 4), (0, 4), (0, 4), (0, 4), (0, 4), (), ())
TRANSPOSED_EARLY = 10
VECTOR_SUMS = (1, 4, 6, 8, 10)
SCALAR_SUMS = (2, 12)
JOB_TILES = 8
JOB_FIRST = 1
STORE_LAG = 2
FINISH_AT = 0
CUT_AT = 0
SHARES = (0, 0, 0, 4, 4, 4, 4, 4, 4, 4)
QUANTISE_AT = 4
SUM_COLS = 256


def flat(ap):
    return ap.rearrange("p a k -> p (a k)")


def words4(ap):
    return ap.rearrange("p a c t -> p (a c t)")


def tile_bitlinear_kernel(tc, x, weight, bias, out):
    nc = tc.nc
    with ExitStack() as ctx:
        keep = ctx.enter_context(tc.tile_pool(name="keep", bufs=1))
        w_pool = ctx.enter_context(tc.tile_pool(name="w", bufs=11))
        abs_pool = ctx.enter_context(tc.tile_pool(name="absolute", bufs=3))
        spare_pool = ctx.enter_context(tc.tile_pool(name="spare", bufs=1))
        q_pool = ctx.enter_context(tc.tile_pool(name="q", bufs=4))
        res_pool = ctx.enter_context(tc.tile_pool(name="res", bufs=16))
        psum = ctx.enter_context(tc.psum_pool(name="psum", bufs=7))
        psum_s = ctx.enter_context(tc.psum_pool(name="psum_s", bufs=1))
        ctx.enter_context(tc.manual_schedule())

        ident = keep.tile([P, P], F32)
        make_identity(nc, ident[:])
        averager = keep.tile([P, P], F32)
        nc.vector.memset(averager[:], 1.0 / (N * K))
        averager_b = keep.tile([P, P], BF16)
        nc.vector.memset(averager_b[:], 1.0 / (N * K))

        starts = [sum(CHUNKS[:c]) for c in range(len(CHUNKS))]
        w_rows = []
        w_place = []
        w_source = []
        for c, width in enumerate(CHUNKS):
            rows = weight[starts[c] : starts[c] + width, :]
            per = width // P
            view = rows.rearrange("(p b) k -> p b k", b=per)
            for i in range(width // PIECE):
                w_rows.append(w_pool.tile([P, 2, K], BF16, tag="w", name="w%d" % len(w_rows)))
                w_place.append((c, PIECE * i))
                w_source.append(view[:, 2 * i : 2 * i + 2, :])
        x_rows = [keep.tile([P, 2, K], BF16, name="x%d" % i) for i in range(M // PIECE)]
        x_view = x.rearrange("(i b p) k -> i p b k", b=2, p=P)
        bias_all = keep.tile([P, N], BF16)

        def load_w(i):
            nc.sync.dma_start(out=w_rows[i][:], in_=w_source[i])

        def load_x(i):
            nc.sync.dma_start(out=x_rows[i][:], in_=x_view[i])

        for i in range(N_PIECES):
            load_w(i)
        load_x(0)
        load_x(1)
        nc.sync.dma_start(out=bias_all[:], in_=bias.partition_broadcast(P))
        load_x(2)
        load_x(3)

        def transpose_piece(rows, grouped, col, leave):
            for g in range(PASSES):
                bank = psum.tile([P, 512], F32, tag="bank")
                planes = bank[:].rearrange("p (u c) -> p u c", u=2)
                for u in range(2):
                    first = (2 * g + u) * P
                    for b in range(2):
                        words = rows[:, b, :].bitcast(F32)
                        nc.tensor.transpose(
                            planes[:, u, P * b : P * (b + 1)], words[:, first : first + P], ident[:]
                        )
                leave(grouped[:, g, col : col + PIECE, :], planes)

        def leave_unchanged(out, planes):
            nc.scalar.copy(out=out.bitcast(F32), in_=planes.rearrange("p u c -> p c u"))

        w_grouped = [
            keep.tile([P, PASSES, width, 4], BF16, name="wt%d" % c, align_bytes=64)
            for c, width in enumerate(CHUNKS)
        ]
        x_grouped = [
            keep.tile([P, PASSES, X_GROUP, 4], BF16, name="xt%d" % i, align_bytes=64) for i in range(X_GROUPS)
        ]
        x_codes = [
            keep.tile([P, PASSES, X_GROUP], U32, name="xc%d" % i, align_bytes=64) for i in range(X_GROUPS)
        ]
        x_scales = [
            keep.tile([P, PASSES, X_GROUP], U8, name="xs%d" % i, align_bytes=64) for i in range(X_GROUPS)
        ]

        def transpose_x(i):
            for half in range(2):
                transpose_piece(x_rows[2 * i + half], x_grouped[i], PIECE * half, leave_unchanged)

        def quantise(grouped, codes, scales):
            nc.vector.quantize_mx(
                out=flat(codes[:]).bitcast(FP8X4), scales=flat(scales[:]), in_=words4(grouped[:])
            )

        sums = psum_s.tile([P, 512], F32, tag="sums")
        sum_rest = keep.tile([P, N_PIECES], F32)
        absolutes = {}

        def clear_signs(i, rows):
            absolute = abs_pool.tile([P, 2, K], BF16, tag="absolute")
            nc.vector.tensor_scalar(
                out=flat(absolute[:, 0:rows, :]).bitcast(I32),
                in0=flat(w_rows[i][:, 0:rows, :]).bitcast(I32),
                scalar1=ABS_BITS,
                scalar2=None,
                op0=ALU.bitwise_and,
            )
            absolutes[i] = flat(absolute[:, 0:rows, :])

        def add_on_tensor(i, first, last):
            steps = absolutes[i].shape[1] // SUM_COLS
            for s in range(steps):
                nc.tensor.matmul(
                    sums[:, 0:SUM_COLS],
                    lhsT=averager_b[:],
                    rhs=absolutes[i][:, SUM_COLS * s : SUM_COLS * (s + 1)],
                    start=(first and s == 0),
                    stop=(last and s == steps - 1),
                )

        def add_on_vector(i, column):
            nc.vector.tensor_scalar(
                out=absolutes[i],
                in0=absolutes[i],
                scalar1=0.0,
                scalar2=None,
                op0=ALU.max,
                op1=ALU.add,
                accum_out=sum_rest[:, column : column + 1],
            )

        def add_on_scalar(i, row, column):
            spare = spare_pool.tile([P, 2, K], BF16, tag="spare")
            nc.scalar.activation(
                out=spare[:, row:2, :],
                in_=w_rows[i][:, row:2, :],
                func=ACT.Abs,
                accum_out=sum_rest[:, column : column + 1],
            )

        def transpose_w(i, leave):
            chunk, col = w_place[i]
            transpose_piece(w_rows[i], w_grouped[chunk], col, leave)

        final = N_PIECES - 1
        rest = 0
        for i in range(final):
            if i not in SCALAR_SUMS:
                clear_signs(i, 2)
            if i < TRANSPOSED_EARLY:
                transpose_w(i, leave_unchanged)
            if i in SCALAR_SUMS:
                add_on_scalar(i, 0, rest)
                rest += 1
            elif i in VECTOR_SUMS:
                add_on_vector(i, rest)
                rest += 1
            else:
                add_on_tensor(i, i == 0, False)
        clear_signs(final, 1)
        add_on_scalar(final, 1, rest)
        rest += 1
        add_on_tensor(final, False, True)

        used = SUM_COLS + rest
        nc.tensor.matmul(sums[:, SUM_COLS:used], lhsT=averager[:], rhs=sum_rest[:, 0:rest], start=True, stop=True)
        mean = keep.tile([P, 1], F32)
        nc.vector.tensor_reduce(out=mean[:], in_=sums[:, 0:used], axis=mybir.AxisListType.X, op=ALU.add)
        half_thr = keep.tile([P, 1], F32)
        nc.vector.tensor_scalar(
            out=half_thr[:], in0=mean[:], scalar1=EPS, scalar2=THRESHOLD / 2, op0=ALU.max, op1=ALU.mult
        )
        half_edge = keep.tile([P, 1], F32)
        nc.vector.tensor_scalar(
            out=half_edge[:].bitcast(I32),
            in0=half_thr[:].bitcast(I32),
            scalar1=TOP_BITS,
            scalar2=THREE_QUARTERS,
            op0=ALU.bitwise_and,
            op1=ALU.bitwise_or,
        )
        stretch = keep.tile([P, 1], F32)
        nc.vector.reciprocal(out=stretch[:], in_=half_edge[:])

        def quarters(c, first, count):
            view = words4(w_grouped[c][:])
            size = view.shape[1] // 4
            return view[:, size * first : size * (first + count)]

        def stretch_on_vector(c, first=0, count=4):
            view = quarters(c, first, count)
            nc.vector.tensor_scalar(out=view, in0=view, scalar1=stretch[:, 0:1], scalar2=None, op0=ALU.mult)

        def stretch_on_scalar(c, first, count=1):
            view = quarters(c, first, count)
            nc.scalar.activation(out=view, in_=view, func=ACT.Copy, scale=stretch[:, 0:1])

        def cut(c):
            view = words4(w_grouped[c][:]).bitcast(I32)
            nc.vector.tensor_scalar(out=view, in0=view, scalar1=TWO_BITS, scalar2=None, op0=ALU.bitwise_and)

        q_codes = {}
        q_scales = {}

        def quantise_q(c):
            codes = q_pool.tile([P, PASSES, CHUNKS[c]], U32, tag="codes", align_bytes=64)
            scales = q_pool.tile([P, PASSES, CHUNKS[c]], U8, tag="scales", align_bytes=64)
            quantise(w_grouped[c], codes, scales)
            q_codes[c] = codes
            q_scales[c] = scales

        def multiply(c, m, on_scalar):
            width = CHUNKS[c]
            per = width // P
            cols = slice(starts[c], starts[c] + width)
            i = m * P // X_GROUP
            rows = slice(m * P - i * X_GROUP, m * P - i * X_GROUP + P)
            acc = psum.tile([P, 512], F32, tag="bank")
            for g in range(PASSES):
                nc.tensor.matmul_mx(
                    out=acc[:, 0:width],
                    lhsT=x_codes[i][:, g, rows].bitcast(FP8X4),
                    lhsT_scale=x_scales[i][:, g, rows],
                    rhs=q_codes[c][:, g, :].bitcast(FP8X4),
                    rhs_scale=q_scales[c][:, g, :],
                    start=(g == 0),
                    stop=(g == PASSES - 1),
                )
            res = res_pool.tile([P, 512], F32, tag="res")
            in_order = acc[:, 0:width].rearrange("p (b r) -> p r b", b=per)
            result = res[:, 0:width].rearrange("p (r b) -> p r b", b=per)
            if on_scalar:
                nc.scalar.activation(out=result, in_=in_order, func=ACT.Copy, scale=0.5)
                nc.gpsimd.tensor_tensor(
                    out=res[:, 0:width], in0=res[:, 0:width], in1=bias_all[:, cols], op=ALU.add
                )
            else:
                nc.vector.scalar_tensor_tensor(
                    out=result,
                    in0=in_order,
                    scalar=0.5,
                    in1=bias_all[:, cols].rearrange("p (r b) -> p r b", b=per),
                    op0=ALU.mult,
                    op1=ALU.add,
                )
            stores.append((STORE_LAG if on_scalar else 0, out[P * m : P * (m + 1), cols], res[:, 0:width]))
            flush(1)

        stores = []

        def flush(age):
            waiting = [(lag - age, place, result) for lag, place, result in stores if lag > 0]
            for lag, place, result in stores:
                if lag <= 0:
                    nc.sync.dma_start(out=place, in_=result)
            stores.clear()
            stores.extend(waiting)

        last = len(CHUNKS) - 1
        per_group = X_GROUP // P
        m_tiles = M // P
        late = list(range(TRANSPOSED_EARLY, N_PIECES))

        def leave_stretched(out, planes):
            nc.scalar.activation(
                out=out.rearrange("p c (u e) -> p c u e", u=2),
                in_=planes.bitcast(BF16).rearrange("p u (c e) -> p c u e", e=2),
                func=ACT.Copy,
                scale=stretch[:, 0:1],
            )

        def scalar_jobs(c):
            pieces = [i for i in late if w_place[i][0] == c]
            if pieces:
                return [(transpose_w, i, leave_stretched) for i in pieces]
            return [(stretch_on_scalar, c, part) for part in range(SHARES[c])]

        def stretch_chunk(c):
            for job, one, two in scalar_jobs(c):
                job(one, two)

        def finish_chunk(c):
            if SHARES[c] < 4:
                stretch_on_vector(c, SHARES[c], 4 - SHARES[c])

        early, later = range(per_group), range(per_group, m_tiles)
        for c in (0, 1):
            stretch_on_vector(c)
        for c in (0, 1):
            cut(c)
        transpose_x(0)
        transpose_x(1)
        for c in (0, 1):
            quantise_q(c)
        quantise(x_grouped[0], x_codes[0], x_scales[0])
        stretch_chunk(2)
        finish_chunk(2)
        for m in early:
            multiply(0, m, False)
        quantise(x_grouped[1], x_codes[1], x_scales[1])
        for m in early:
            multiply(1, m, False)
        stretch_chunk(3)
        cut(2)
        for m in later:
            multiply(0, m, False)
        quantise_q(2)
        for m in later:
            multiply(1, m, False)
        stretch_chunk(4)
        for c in range(2, last + 1):
            jobs = scalar_jobs(c + 3) if c + 3 <= last else []
            step = JOB_TILES // max(1, len(jobs))
            for m in range(m_tiles):
                if jobs and m % step == JOB_FIRST:
                    job, one, two = jobs.pop(0)
                    job(one, two)
                multiply(c, m, m in SCALAR_TILES[c])
                if m == FINISH_AT and c + 1 <= last:
                    finish_chunk(c + 1)
                if m == CUT_AT and c + 1 <= last:
                    cut(c + 1)
                if m == QUANTISE_AT and c + 1 <= last:
                    quantise_q(c + 1)
        flush(1)
        while stores:
            flush(1)
